import numpy as np
import ml_dtypes


def mxq(x, axis, fmt="e4m3"):
    dtype, down = {"e4m3": (ml_dtypes.float8_e4m3fn, 7), "e5m2": (ml_dtypes.float8_e5m2, 14)}[fmt]
    v = np.moveaxis(np.asarray(x, np.float32).astype(ml_dtypes.bfloat16).astype(np.float64), axis, -1)
    blocks = v.reshape(v.shape[:-1] + (-1, 32))
    amax = np.abs(blocks).max(-1, keepdims=True)
    byte = np.maximum(np.where(amax > 0, np.frexp(amax)[1] - 1 + 127, 0) - down, 1)
    scale = np.exp2(byte - 127.0)
    codes = (blocks / scale).astype(np.float32).astype(dtype).astype(np.float64)
    return np.moveaxis((codes * scale).reshape(v.shape), -1, axis)


WIDE = False


def mx_kscale(k):
    if not WIDE:
        return np.ones(k)
    levels = np.array([10, -10, 5, -5, 0])
    a = np.random.permutation(np.resize(levels, k // 512 * 4)).reshape(k // 512, 4)
    idx = np.arange(k)
    return np.exp2(a[idx // 512, idx % 128 // 32])


BF16 = ml_dtypes.bfloat16


def bf(x):
    return np.asarray(x, np.float32).astype(BF16)


def f64(x):
    return np.asarray(x).astype(np.float64)


B, M, D, N, P, H = 32, 1024, 512, 8, 16, 1024
R = B * P


def silu(v):
    return v / (1.0 + np.exp(-v))


def setup_inputs():
    s = mx_kscale(D)
    return {"xs_mix": bf(np.random.standard_normal((B, N, P, D)) * 0.3 / np.sqrt(D) * s),
            "task_emb": bf(np.random.standard_normal((P, D)) * 0.5 / np.sqrt(D) * s),
            "W1": bf(np.random.standard_normal((N, D, H)) * 2.0 / s[:, None]),
            "b1": bf(np.random.standard_normal((N, H)) * 0.3),
            "W2": bf(np.random.standard_normal((N, H, D)) / np.sqrt(H * D) * s),
            "b2": bf(np.random.standard_normal((N, D)) * 0.3 / np.sqrt(D) * s),
            "ln_g": bf(1.0 + 0.1 * np.random.standard_normal((N, D))),
            "ln_b": bf(0.1 * np.random.standard_normal((N, D)))}


def reference(xs_mix, task_emb, W1, b1, W2, b2, ln_g, ln_b):
    xs = f64(xs_mix) + f64(task_emb)[None, None, :, :]
    xe = xs.transpose(1, 0, 2, 3).reshape(N, R, D)
    h = silu((mxq(xe, 2, "e4m3") @ mxq(f64(W1), 1, "e4m3")) + f64(b1)[:, None, :])
    mlp = (mxq(h, 2, "e4m3") @ mxq(f64(W2), 1, "e4m3")) + f64(b2)[:, None, :]
    r = xe + mlp
    mu = r.mean(-1, keepdims=True)
    var = ((r - mu) ** 2).mean(-1, keepdims=True)
    ys = (r - mu) / np.sqrt(var + 1e-5) * f64(ln_g)[:, None, :] + f64(ln_b)[:, None, :]
    return ys.reshape(N, B, P, D).transpose(1, 0, 2, 3)

@@ -1,0 +1,270 @@
+from contextlib import ExitStack
+
+import concourse.mybir as mybir
+from concourse.masks import make_identity
+
+F32 = mybir.dt.float32
+BF16 = mybir.dt.bfloat16
+U32 = mybir.dt.uint32
+U8 = mybir.dt.uint8
+FP8X4 = mybir.dt.float8_e4m3fn_x4
+ALU = mybir.AluOpType
+ACT = mybir.ActivationFunctionType
+
+P = 128
+PACK = 4
+K_PASS = P * PACK
+
+BATCH, EXPERTS, TASKS, D, H = 32, 8, 16, 512, 1024
+ROWS = BATCH * TASKS
+ROW_TILES = ROWS // P
+TASKS_PER_TILE = P // BATCH
+B2_ROW = 32
+H_TILES = H // P
+H_PASSES = H // K_PASS
+LN_EPS = 1e-5
+
+FLOPS = 2 * EXPERTS * ROWS * (D * H + H * D)
+
+
+def regroup(copy, grouped, planes):
+    copy(
+        out=grouped.rearrange("p (c i) t -> p c t i", i=4),
+        in_=planes.rearrange("p t (c i) -> p c t i", i=4),
+    )
+
+
+def tile_hdmodel_pb_t_kernel(tc, xs_mix, task_emb, W1, b1, W2, b2, ln_g, ln_b, out):
+    nc = tc.nc
+    with ExitStack() as ctx:
+        const = ctx.enter_context(tc.tile_pool(name="const", bufs=1))
+        loads = ctx.enter_context(tc.tile_pool(name="loads", bufs=2))
+        vectors = ctx.enter_context(tc.tile_pool(name="vectors", bufs=4))
+        grouped_w = ctx.enter_context(tc.tile_pool(name="grouped_w", bufs=1))
+        operands = ctx.enter_context(tc.tile_pool(name="operands", bufs=2))
+        work = ctx.enter_context(tc.tile_pool(name="work", bufs=2))
+        norm = ctx.enter_context(tc.tile_pool(name="norm", bufs=4))
+        psum_t = ctx.enter_context(tc.psum_pool(name="psum_t", bufs=2))
+        psum_h = ctx.enter_context(tc.psum_pool(name="psum_h", bufs=3))
+        psum_o = ctx.enter_context(tc.psum_pool(name="psum_o", bufs=2))
+        psum_s = ctx.enter_context(tc.psum_pool(name="psum_s", bufs=1))
+
+        ident = const.tile([P, P], BF16)
+        make_identity(nc, ident[:])
+        neg_half = const.tile([P, 1], F32)
+        nc.vector.memset(neg_half[:], -0.5)
+
+        def task_rows(dram_bpd, j):
+            return dram_bpd.rearrange("b (i j) d -> j b i d", j=TASKS_PER_TILE)[j]
+
+        te_rep = const.tile([P, ROW_TILES, D], BF16)
+        for j in range(TASKS_PER_TILE):
+            nc.scalar.dma_start(
+                out=te_rep[j:P:TASKS_PER_TILE, :, :],
+                in_=task_rows(task_emb.unsqueeze(0).to_broadcast([BATCH, TASKS, D]), j),
+            )
+
+        addends = const.tile([P, EXPERTS, D], BF16)
+        nc.vector.memset(addends[:], 0.0)
+        nc.scalar.dma_start(
+            out=addends[0:TASKS, :, :], in_=task_emb.unsqueeze(1).to_broadcast([TASKS, EXPERTS, D])
+        )
+        nc.scalar.dma_start(out=addends[B2_ROW : B2_ROW + 1, :, :], in_=b2.unsqueeze(0))
+        select = const.tile([P, ROW_TILES, P], BF16)
+        nc.vector.tensor_copy(
+            out=select[:].rearrange("k i (b j) -> k i b j", j=TASKS_PER_TILE),
+            in_=ident[:, 0:TASKS]
+            .rearrange("k (i j) -> k i j", j=TASKS_PER_TILE)
+            .unsqueeze(2)
+            .to_broadcast([P, ROW_TILES, BATCH, TASKS_PER_TILE]),
+        )
+        nc.vector.memset(select[B2_ROW : B2_ROW + 1, :, :], 1.0)
+
+        b1_rows = const.tile([P, P], BF16)
+        nc.vector.memset(b1_rows[:], 0.0)
+        nc.scalar.dma_start(
+            out=b1_rows[0 : EXPERTS * H_TILES, :], in_=b1.rearrange("n (m q) -> (n m) q", q=P)
+        )
+        b1_t = psum_t.tile([P, P], BF16, tag="xt")
+        nc.tensor.transpose(b1_t[:], b1_rows[:], ident[:])
+        b1_cols = const.tile([P, EXPERTS * H_TILES], F32)
+        nc.vector.tensor_copy(out=b1_cols[:], in_=b1_t[:, 0 : EXPERTS * H_TILES])
+
+        loaded = {}
+        ready = {}
+        hidden = {}
+
+        def load(n):
+            xm = loads.tile([P, ROW_TILES, D], BF16)
+            for j in range(TASKS_PER_TILE):
+                nc.sync.dma_start(out=xm[j:P:TASKS_PER_TILE, :, :], in_=task_rows(xs_mix[:, n], j))
+            w1_raw = loads.tile([P, PACK, H], BF16)
+            nc.sync.dma_start(out=w1_raw[:], in_=W1[n].rearrange("(t p) h -> p t h", p=P))
+            w2_raw = loads.tile([P, H_PASSES, PACK, D], BF16)
+            nc.sync.dma_start(
+                out=w2_raw[:], in_=W2[n].rearrange("(c t p) d -> p c t d", t=PACK, p=P)
+            )
+            gain_bc = vectors.tile([P, D], BF16)
+            nc.sync.dma_start(out=gain_bc[:], in_=ln_g[n].partition_broadcast(P))
+            beta_bc = vectors.tile([P, D], BF16)
+            nc.sync.dma_start(out=beta_bc[:], in_=ln_b[n].partition_broadcast(P))
+            loaded[n] = (xm, w1_raw, w2_raw, gain_bc, beta_bc)
+
+        def prepare(n):
+            xm, w1_raw, w2_raw, gain_bc, beta_bc = loaded[n]
+
+            xs_bf = work.tile([P, ROW_TILES, D], BF16)
+            nc.vector.tensor_tensor(out=xs_bf[:], in0=xm[:], in1=te_rep[:], op=ALU.add)
+
+            w1_grouped = grouped_w.tile([P, H, PACK], BF16, align_bytes=64)
+            w1_codes = operands.tile([P, H], U32, align_bytes=64)
+            w1_scales = operands.tile([P, H], U8, align_bytes=64)
+            half_h = H // 2
+            for s in range(2):
+                cols = slice(s * half_h, (s + 1) * half_h)
+                regroup(nc.vector.tensor_copy, w1_grouped[:, cols, :], w1_raw[:, :, cols])
+            for s in range(2):
+                cols = slice(s * half_h, (s + 1) * half_h)
+                nc.vector.quantize_mx(
+                    out=w1_codes[:, cols].bitcast(FP8X4),
+                    scales=w1_scales[:, cols],
+                    in_=w1_grouped[:, cols, :].rearrange("p w t -> p (w t)"),
+                )
+
+            x_grouped = work.tile([P, ROWS, PACK], BF16, align_bytes=64)
+            for pair in range(ROW_TILES // 2):
+                xt = psum_t.tile([P, 2, PACK, P], BF16, tag="xt")
+                for i in range(2):
+                    for t in range(PACK):
+                        nc.tensor.transpose(
+                            xt[:, i, t, :], xs_bf[:, 2 * pair + i, t * P : (t + 1) * P], ident[:]
+                        )
+                nc.scalar.copy(
+                    out=x_grouped[:, 2 * pair * P : (2 * pair + 2) * P, :].rearrange(
+                        "p (i r) t -> p i r t", i=2
+                    ),
+                    in_=xt[:].rearrange("p i t r -> p i r t"),
+                )
+
+            w2_grouped = grouped_w.tile([P, H_PASSES, D, PACK], BF16, align_bytes=64)
+            w2_codes = operands.tile([P, H_PASSES, D], U32, align_bytes=64, bufs=3)
+            w2_scales = operands.tile([P, H_PASSES, D], U8, align_bytes=64, bufs=3)
+            for c in range(H_PASSES):
+                regroup(nc.scalar.copy, w2_grouped[:, c, :, :], w2_raw[:, c, :, :])
+
+            x_codes = operands.tile([P, ROWS], U32, align_bytes=64)
+            x_scales = operands.tile([P, ROWS], U8, align_bytes=64)
+            nc.vector.quantize_mx(
+                out=x_codes[:].bitcast(FP8X4),
+                scales=x_scales[:],
+                in_=x_grouped[:].rearrange("p r t -> p (r t)"),
+            )
+
+            resid = work.tile([P, ROW_TILES, D], F32, bufs=3)
+            for i in range(ROW_TILES):
+                shift = psum_s.tile([P, D], F32)
+                nc.tensor.matmul(out=shift[:], lhsT=select[:, i, :], rhs=addends[:, n, :], start=True, stop=True)
+                nc.vector.tensor_tensor(out=resid[:, i, :], in0=shift[:], in1=xm[:, i, :], op=ALU.add)
+
+            for c in range(H_PASSES):
+                nc.vector.quantize_mx(
+                    out=w2_codes[:, c, :].bitcast(FP8X4),
+                    scales=w2_scales[:, c, :],
+                    in_=w2_grouped[:, c, :, :].rearrange("p w t -> p (w t)"),
+                )
+            ready[n] = (w1_codes, w1_scales, x_codes, x_scales, w2_codes, w2_scales, resid, gain_bc, beta_bc)
+
+        def first_layer(n):
+            w1_codes, w1_scales, x_codes, x_scales = ready[n][0:4]
+
+            h_t = work.tile([P, H_TILES, ROWS], BF16)
+            h_codes = operands.tile([P, H_PASSES, ROWS], U32, align_bytes=64)
+            h_scales = operands.tile([P, H_PASSES, ROWS], U8, align_bytes=64)
+            for c in range(H_PASSES):
+                for t in range(PACK):
+                    m = c * PACK + t
+                    units = slice(m * P, (m + 1) * P)
+                    pre = psum_h.tile([P, ROWS], F32)
+                    nc.tensor.matmul_mx(
+                        out=pre[:],
+                        lhsT=w1_codes[:, units].bitcast(FP8X4),
+                        lhsT_scale=w1_scales[:, units],
+                        rhs=x_codes[:].bitcast(FP8X4),
+                        rhs_scale=x_scales[:],
+                        start=True,
+                        stop=True,
+                    )
+                    col = n * H_TILES + m
+                    nc.scalar.activation(
+                        out=h_t[:, m, :], in_=pre[:], func=ACT.Silu, bias=b1_cols[:, col : col + 1], scale=1.0
+                    )
+                h_grouped = work.tile([P, ROWS, PACK], BF16, align_bytes=64)
+                regroup(nc.scalar.copy, h_grouped[:], h_t[:, c * PACK : (c + 1) * PACK, :])
+                nc.vector.quantize_mx(
+                    out=h_codes[:, c, :].bitcast(FP8X4),
+                    scales=h_scales[:, c, :],
+                    in_=h_grouped[:].rearrange("p r t -> p (r t)"),
+                )
+
+            hidden[n] = (h_codes, h_scales)
+
+        def second_layer(n):
+            w2_codes, w2_scales, resid, gain_bc, beta_bc = ready[n][4:9]
+            h_codes, h_scales = hidden[n]
+
+            y = work.tile([P, ROW_TILES, D], F32)
+            for i in range(ROW_TILES):
+                rows = slice(i * P, (i + 1) * P)
+                mlp = psum_o.tile([P, D], F32)
+                for c in range(H_PASSES):
+                    nc.tensor.matmul_mx(
+                        out=mlp[:],
+                        lhsT=h_codes[:, c, rows].bitcast(FP8X4),
+                        lhsT_scale=h_scales[:, c, rows],
+                        rhs=w2_codes[:, c, :].bitcast(FP8X4),
+                        rhs_scale=w2_scales[:, c, :],
+                        start=(c == 0),
+                        stop=(c == H_PASSES - 1),
+                    )
+                r = norm.tile([P, D], F32)
+                r_sum = norm.tile([P, 1], F32)
+                nc.vector.scalar_tensor_tensor(
+                    out=r[:], in0=mlp[:], scalar=1.0, in1=resid[:, i, :], op0=ALU.mult, op1=ALU.add, accum_out=r_sum[:]
+                )
+                neg_mean = norm.tile([P, 1], F32)
+                nc.gpsimd.tensor_scalar(
+                    out=neg_mean[:], in0=r_sum[:], scalar1=-1.0 / D, scalar2=0.0, op0=ALU.mult, op1=ALU.add
+                )
+                squares = norm.tile([P, D], BF16)
+                sq_sum = norm.tile([P, 1], F32)
+                nc.scalar.activation(
+                    out=squares[:], in_=r[:], func=ACT.Square, bias=neg_mean[:], scale=1.0, accum_out=sq_sum[:]
+                )
+                centred_gain = norm.tile([P, D], F32)
+                nc.vector.scalar_tensor_tensor(
+                    out=centred_gain[:], in0=r[:], scalar=neg_mean[:], in1=gain_bc[:], op0=ALU.add, op1=ALU.mult
+                )
+                var_eps = norm.tile([P, 1], F32)
+                nc.gpsimd.tensor_scalar(
+                    out=var_eps[:], in0=sq_sum[:], scalar1=1.0 / D, scalar2=LN_EPS, op0=ALU.mult, op1=ALU.add
+                )
+                rstd = norm.tile([P, 1], F32)
+                nc.gpsimd.tensor_tensor(out=rstd[:], in0=var_eps[:], in1=neg_half[:], op=ALU.pow)
+                nc.vector.scalar_tensor_tensor(
+                    out=y[:, i, :], in0=centred_gain[:], scalar=rstd[:], in1=beta_bc[:], op0=ALU.mult, op1=ALU.add
+                )
+            for j in range(TASKS_PER_TILE):
+                nc.sync.dma_start(out=task_rows(out[:, n], j), in_=y[j:P:TASKS_PER_TILE, :, :])
+
+        load(0)
+        load(1)
+        prepare(0)
+        for n in range(EXPERTS + 1):
+            if n + 2 < EXPERTS:
+                load(n + 2)
+            if n >= 1:
+                second_layer(n - 1)
+            if n < EXPERTS:
+                first_layer(n)
+            if n + 1 < EXPERTS:
+                prepare(n + 1)

@@ -20,6 +20,8 @@ ROWS = BATCH * TASKS
 ROW_TILES = ROWS // P
 TASKS_PER_TILE = P // BATCH
 B2_ROW = 32
+HALVES = 2
+TILES_PER_HALF = ROW_TILES // HALVES
 H_TILES = H // P
 H_PASSES = H // K_PASS
 LN_EPS = 1e-5
@@ -40,18 +42,18 @@ def tile_hdmodel_pb_t_kernel(tc, xs_mix, task_emb, W1, b1, W2, b2, ln_g, ln_b, o
         const = ctx.enter_context(tc.tile_pool(name="const", bufs=1))
         loads = ctx.enter_context(tc.tile_pool(name="loads", bufs=2))
         vectors = ctx.enter_context(tc.tile_pool(name="vectors", bufs=4))
-        grouped_w = ctx.enter_context(tc.tile_pool(name="grouped_w", bufs=1))
-        operands = ctx.enter_context(tc.tile_pool(name="operands", bufs=2))
-        work = ctx.enter_context(tc.tile_pool(name="work", bufs=2))
-        norm = ctx.enter_context(tc.tile_pool(name="norm", bufs=4))
-        psum_t = ctx.enter_context(tc.psum_pool(name="psum_t", bufs=2))
+        single = ctx.enter_context(tc.tile_pool(name="single", bufs=1))
+        double = ctx.enter_context(tc.tile_pool(name="double", bufs=2))
+        norm = ctx.enter_context(tc.tile_pool(name="norm", bufs=ROW_TILES))
+        psum_t = ctx.enter_context(tc.psum_pool(name="psum_t", bufs=1))
         psum_h = ctx.enter_context(tc.psum_pool(name="psum_h", bufs=3))
         psum_o = ctx.enter_context(tc.psum_pool(name="psum_o", bufs=2))
-        psum_s = ctx.enter_context(tc.psum_pool(name="psum_s", bufs=1))
+        psum_s = ctx.enter_context(tc.psum_pool(name="psum_s", bufs=2))
+        ctx.enter_context(tc.manual_schedule())
 
         ident = const.tile([P, P], BF16)
         make_identity(nc, ident[:])
-        neg_half = const.tile([P, 1], F32)
+        neg_half = const.tile([P, TILES_PER_HALF], F32)
         nc.vector.memset(neg_half[:], -0.5)
 
         def task_rows(dram_bpd, j):
@@ -63,6 +65,31 @@ def tile_hdmodel_pb_t_kernel(tc, xs_mix, task_emb, W1, b1, W2, b2, ln_g, ln_b, o
                 out=te_rep[j:P:TASKS_PER_TILE, :, :],
                 in_=task_rows(task_emb.unsqueeze(0).to_broadcast([BATCH, TASKS, D]), j),
             )
+
+        tiles = {}
+
+        def load(n):
+            xm = loads.tile([P, ROW_TILES, D], BF16)
+            for j in range(TASKS_PER_TILE):
+                nc.sync.dma_start(out=xm[j:P:TASKS_PER_TILE, :, :], in_=task_rows(xs_mix[:, n], j))
+            w1_raw = loads.tile([P, PACK, H], BF16)
+            nc.sync.dma_start(out=w1_raw[:], in_=W1[n].rearrange("(t p) h -> p t h", p=P))
+            w2_raw = loads.tile([P, H_PASSES, PACK, D], BF16)
+            nc.sync.dma_start(
+                out=w2_raw[:], in_=W2[n].rearrange("(c t p) d -> p c t d", t=PACK, p=P)
+            )
+            gain_bc = vectors.tile([P, D], BF16)
+            nc.sync.dma_start(out=gain_bc[:], in_=ln_g[n].partition_broadcast(P))
+            beta_bc = vectors.tile([P, D], BF16)
+            nc.sync.dma_start(out=beta_bc[:], in_=ln_b[n].partition_broadcast(P))
+            tiles["xm", n] = xm
+            tiles["w1_raw", n] = w1_raw
+            tiles["w2_raw", n] = w2_raw
+            tiles["gain", n] = gain_bc
+            tiles["beta", n] = beta_bc
+
+        load(0)
+        load(1)
 
         addends = const.tile([P, EXPERTS, D], BF16)
         nc.vector.memset(addends[:], 0.0)
@@ -85,44 +112,54 @@ def tile_hdmodel_pb_t_kernel(tc, xs_mix, task_emb, W1, b1, W2, b2, ln_g, ln_b, o
         nc.scalar.dma_start(
             out=b1_rows[0 : EXPERTS * H_TILES, :], in_=b1.rearrange("n (m q) -> (n m) q", q=P)
         )
-        b1_t = psum_t.tile([P, P], BF16, tag="xt")
-        nc.tensor.transpose(b1_t[:], b1_rows[:], ident[:])
         b1_cols = const.tile([P, EXPERTS * H_TILES], F32)
-        nc.vector.tensor_copy(out=b1_cols[:], in_=b1_t[:, 0 : EXPERTS * H_TILES])
 
-        loaded = {}
-        ready = {}
-        hidden = {}
+        def transpose_b1():
+            b1_t = psum_s.tile([P, P], BF16, tag="shift")
+            nc.tensor.transpose(b1_t[:], b1_rows[:], ident[:])
+            nc.vector.tensor_copy(out=b1_cols[:], in_=b1_t[:, 0 : EXPERTS * H_TILES])
 
-        def load(n):
-            xm = loads.tile([P, ROW_TILES, D], BF16)
-            for j in range(TASKS_PER_TILE):
-                nc.sync.dma_start(out=xm[j:P:TASKS_PER_TILE, :, :], in_=task_rows(xs_mix[:, n], j))
-            w1_raw = loads.tile([P, PACK, H], BF16)
-            nc.sync.dma_start(out=w1_raw[:], in_=W1[n].rearrange("(t p) h -> p t h", p=P))
-            w2_raw = loads.tile([P, H_PASSES, PACK, D], BF16)
-            nc.sync.dma_start(
-                out=w2_raw[:], in_=W2[n].rearrange("(c t p) d -> p c t d", t=PACK, p=P)
+        def add_task_embedding(n):
+            xs_bf = double.tile([P, ROW_TILES, D], BF16)
+            nc.vector.tensor_tensor(out=xs_bf[:], in0=tiles["xm", n][:], in1=te_rep[:], op=ALU.add)
+            x_grouped = double.tile([P, ROWS, PACK], BF16, align_bytes=64)
+            tiles["xs_bf", n] = xs_bf
+            tiles["x_grouped", n] = x_grouped
+
+        def transpose_x(n, half):
+            xt = psum_t.tile([P, TILES_PER_HALF, PACK, P], BF16, tag="xt")
+            for i in range(TILES_PER_HALF):
+                for t in range(PACK):
+                    nc.tensor.transpose(
+                        xt[:, i, t, :],
+                        tiles["xs_bf", n][:, half * TILES_PER_HALF + i, t * P : (t + 1) * P],
+                        ident[:],
+                    )
+            rows = slice(half * TILES_PER_HALF * P, (half + 1) * TILES_PER_HALF * P)
+            nc.scalar.copy(
+                out=tiles["x_grouped", n][:, rows, :].rearrange("p (i r) t -> p i r t", i=TILES_PER_HALF),
+                in_=xt[:].rearrange("p i t r -> p i r t"),
             )
-            gain_bc = vectors.tile([P, D], BF16)
-            nc.sync.dma_start(out=gain_bc[:], in_=ln_g[n].partition_broadcast(P))
-            beta_bc = vectors.tile([P, D], BF16)
-            nc.sync.dma_start(out=beta_bc[:], in_=ln_b[n].partition_broadcast(P))
-            loaded[n] = (xm, w1_raw, w2_raw, gain_bc, beta_bc)
 
-        def prepare(n):
-            xm, w1_raw, w2_raw, gain_bc, beta_bc = loaded[n]
+        def quantise_x(n):
+            x_codes = double.tile([P, ROWS], U32, align_bytes=64)
+            x_scales = double.tile([P, ROWS], U8, align_bytes=64)
+            nc.vector.quantize_mx(
+                out=x_codes[:].bitcast(FP8X4),
+                scales=x_scales[:],
+                in_=tiles["x_grouped", n][:].rearrange("p r t -> p (r t)"),
+            )
+            tiles["x_codes", n] = x_codes
+            tiles["x_scales", n] = x_scales
 
-            xs_bf = work.tile([P, ROW_TILES, D], BF16)
-            nc.vector.tensor_tensor(out=xs_bf[:], in0=xm[:], in1=te_rep[:], op=ALU.add)
-
-            w1_grouped = grouped_w.tile([P, H, PACK], BF16, align_bytes=64)
-            w1_codes = operands.tile([P, H], U32, align_bytes=64)
-            w1_scales = operands.tile([P, H], U8, align_bytes=64)
+        def quantise_w1(n):
+            w1_grouped = single.tile([P, H, PACK], BF16, align_bytes=64)
+            w1_codes = double.tile([P, H], U32, align_bytes=64)
+            w1_scales = double.tile([P, H], U8, align_bytes=64)
             half_h = H // 2
             for s in range(2):
                 cols = slice(s * half_h, (s + 1) * half_h)
-                regroup(nc.vector.tensor_copy, w1_grouped[:, cols, :], w1_raw[:, :, cols])
+                regroup(nc.vector.tensor_copy, w1_grouped[:, cols, :], tiles["w1_raw", n][:, :, cols])
             for s in range(2):
                 cols = slice(s * half_h, (s + 1) * half_h)
                 nc.vector.quantize_mx(
@@ -130,141 +167,209 @@ def tile_hdmodel_pb_t_kernel(tc, xs_mix, task_emb, W1, b1, W2, b2, ln_g, ln_b, o
                     scales=w1_scales[:, cols],
                     in_=w1_grouped[:, cols, :].rearrange("p w t -> p (w t)"),
                 )
+            tiles["w1_codes", n] = w1_codes
+            tiles["w1_scales", n] = w1_scales
 
-            x_grouped = work.tile([P, ROWS, PACK], BF16, align_bytes=64)
-            for pair in range(ROW_TILES // 2):
-                xt = psum_t.tile([P, 2, PACK, P], BF16, tag="xt")
-                for i in range(2):
-                    for t in range(PACK):
-                        nc.tensor.transpose(
-                            xt[:, i, t, :], xs_bf[:, 2 * pair + i, t * P : (t + 1) * P], ident[:]
-                        )
-                nc.scalar.copy(
-                    out=x_grouped[:, 2 * pair * P : (2 * pair + 2) * P, :].rearrange(
-                        "p (i r) t -> p i r t", i=2
-                    ),
-                    in_=xt[:].rearrange("p i t r -> p i r t"),
-                )
+        def regroup_w2(n, c):
+            if c == 0:
+                w2_grouped = single.tile([P, H_PASSES, D, PACK], BF16, align_bytes=64)
+                tiles["w2_grouped", n] = w2_grouped
+            regroup(nc.scalar.copy, tiles["w2_grouped", n][:, c, :, :], tiles["w2_raw", n][:, c, :, :])
 
-            w2_grouped = grouped_w.tile([P, H_PASSES, D, PACK], BF16, align_bytes=64)
-            w2_codes = operands.tile([P, H_PASSES, D], U32, align_bytes=64, bufs=3)
-            w2_scales = operands.tile([P, H_PASSES, D], U8, align_bytes=64, bufs=3)
-            for c in range(H_PASSES):
-                regroup(nc.scalar.copy, w2_grouped[:, c, :, :], w2_raw[:, c, :, :])
-
-            x_codes = operands.tile([P, ROWS], U32, align_bytes=64)
-            x_scales = operands.tile([P, ROWS], U8, align_bytes=64)
-            nc.vector.quantize_mx(
-                out=x_codes[:].bitcast(FP8X4),
-                scales=x_scales[:],
-                in_=x_grouped[:].rearrange("p r t -> p (r t)"),
-            )
-
-            resid = work.tile([P, ROW_TILES, D], F32, bufs=3)
-            for i in range(ROW_TILES):
-                shift = psum_s.tile([P, D], F32)
-                nc.tensor.matmul(out=shift[:], lhsT=select[:, i, :], rhs=addends[:, n, :], start=True, stop=True)
-                nc.vector.tensor_tensor(out=resid[:, i, :], in0=shift[:], in1=xm[:, i, :], op=ALU.add)
-
+        def quantise_w2(n):
+            w2_codes = double.tile([P, H_PASSES, D], U32, align_bytes=64)
+            w2_scales = double.tile([P, H_PASSES, D], U8, align_bytes=64)
             for c in range(H_PASSES):
                 nc.vector.quantize_mx(
                     out=w2_codes[:, c, :].bitcast(FP8X4),
                     scales=w2_scales[:, c, :],
-                    in_=w2_grouped[:, c, :, :].rearrange("p w t -> p (w t)"),
+                    in_=tiles["w2_grouped", n][:, c, :, :].rearrange("p w t -> p (w t)"),
                 )
-            ready[n] = (w1_codes, w1_scales, x_codes, x_scales, w2_codes, w2_scales, resid, gain_bc, beta_bc)
+            tiles["w2_codes", n] = w2_codes
+            tiles["w2_scales", n] = w2_scales
 
-        def first_layer(n):
-            w1_codes, w1_scales, x_codes, x_scales = ready[n][0:4]
-
-            h_t = work.tile([P, H_TILES, ROWS], BF16)
-            h_codes = operands.tile([P, H_PASSES, ROWS], U32, align_bytes=64)
-            h_scales = operands.tile([P, H_PASSES, ROWS], U8, align_bytes=64)
-            for c in range(H_PASSES):
-                for t in range(PACK):
-                    m = c * PACK + t
-                    units = slice(m * P, (m + 1) * P)
-                    pre = psum_h.tile([P, ROWS], F32)
-                    nc.tensor.matmul_mx(
-                        out=pre[:],
-                        lhsT=w1_codes[:, units].bitcast(FP8X4),
-                        lhsT_scale=w1_scales[:, units],
-                        rhs=x_codes[:].bitcast(FP8X4),
-                        rhs_scale=x_scales[:],
-                        start=True,
-                        stop=True,
-                    )
-                    col = n * H_TILES + m
-                    nc.scalar.activation(
-                        out=h_t[:, m, :], in_=pre[:], func=ACT.Silu, bias=b1_cols[:, col : col + 1], scale=1.0
-                    )
-                h_grouped = work.tile([P, ROWS, PACK], BF16, align_bytes=64)
-                regroup(nc.scalar.copy, h_grouped[:], h_t[:, c * PACK : (c + 1) * PACK, :])
-                nc.vector.quantize_mx(
-                    out=h_codes[:, c, :].bitcast(FP8X4),
-                    scales=h_scales[:, c, :],
-                    in_=h_grouped[:].rearrange("p r t -> p (r t)"),
-                )
-
-            hidden[n] = (h_codes, h_scales)
-
-        def second_layer(n):
-            w2_codes, w2_scales, resid, gain_bc, beta_bc = ready[n][4:9]
-            h_codes, h_scales = hidden[n]
-
-            y = work.tile([P, ROW_TILES, D], F32)
+        def residual_addend(n):
+            resid = double.tile([P, ROW_TILES, D], F32)
             for i in range(ROW_TILES):
+                shift = psum_s.tile([P, D], F32)
+                nc.tensor.matmul(out=shift[:], lhsT=select[:, i, :], rhs=addends[:, n, :], start=True, stop=True)
+                nc.vector.tensor_tensor(out=resid[:, i, :], in0=shift[:], in1=tiles["xm", n][:, i, :], op=ALU.add)
+            tiles["resid", n] = resid
+
+        def hidden_units(n, first, count):
+            if first == 0:
+                h_t = single.tile([P, H_TILES, ROWS], BF16)
+                tiles["h_t", n] = h_t
+            for m in range(first, first + count):
+                units = slice(m * P, (m + 1) * P)
+                pre = psum_h.tile([P, ROWS], F32)
+                nc.tensor.matmul_mx(
+                    out=pre[:],
+                    lhsT=tiles["w1_codes", n][:, units].bitcast(FP8X4),
+                    lhsT_scale=tiles["w1_scales", n][:, units],
+                    rhs=tiles["x_codes", n][:].bitcast(FP8X4),
+                    rhs_scale=tiles["x_scales", n][:],
+                    start=True,
+                    stop=True,
+                )
+                col = n * H_TILES + m
+                nc.scalar.activation(
+                    out=tiles["h_t", n][:, m, :], in_=pre[:], func=ACT.Silu, bias=b1_cols[:, col : col + 1], scale=1.0
+                )
+
+        def regroup_h(n, c):
+            h_grouped = double.tile([P, ROWS, PACK], BF16, align_bytes=64)
+            regroup(nc.scalar.copy, h_grouped[:], tiles["h_t", n][:, c * PACK : (c + 1) * PACK, :])
+            tiles["h_grouped", n, c] = h_grouped
+
+        def quantise_h(n, c):
+            if c == 0:
+                h_codes = double.tile([P, H_PASSES, ROWS], U32, align_bytes=64)
+                h_scales = double.tile([P, H_PASSES, ROWS], U8, align_bytes=64)
+                tiles["h_codes", n] = h_codes
+                tiles["h_scales", n] = h_scales
+            nc.vector.quantize_mx(
+                out=tiles["h_codes", n][:, c, :].bitcast(FP8X4),
+                scales=tiles["h_scales", n][:, c, :],
+                in_=tiles["h_grouped", n, c][:].rearrange("p r t -> p (r t)"),
+            )
+
+        def second_product(n, half):
+            r_sum = norm.tile([P, TILES_PER_HALF], F32)
+            for k in range(TILES_PER_HALF):
+                i = half * TILES_PER_HALF + k
                 rows = slice(i * P, (i + 1) * P)
                 mlp = psum_o.tile([P, D], F32)
                 for c in range(H_PASSES):
                     nc.tensor.matmul_mx(
                         out=mlp[:],
-                        lhsT=h_codes[:, c, rows].bitcast(FP8X4),
-                        lhsT_scale=h_scales[:, c, rows],
-                        rhs=w2_codes[:, c, :].bitcast(FP8X4),
-                        rhs_scale=w2_scales[:, c, :],
+                        lhsT=tiles["h_codes", n][:, c, rows].bitcast(FP8X4),
+                        lhsT_scale=tiles["h_scales", n][:, c, rows],
+                        rhs=tiles["w2_codes", n][:, c, :].bitcast(FP8X4),
+                        rhs_scale=tiles["w2_scales", n][:, c, :],
                         start=(c == 0),
                         stop=(c == H_PASSES - 1),
                     )
                 r = norm.tile([P, D], F32)
-                r_sum = norm.tile([P, 1], F32)
                 nc.vector.scalar_tensor_tensor(
-                    out=r[:], in0=mlp[:], scalar=1.0, in1=resid[:, i, :], op0=ALU.mult, op1=ALU.add, accum_out=r_sum[:]
+                    out=r[:],
+                    in0=mlp[:],
+                    scalar=1.0,
+                    in1=tiles["resid", n][:, i, :],
+                    op0=ALU.mult,
+                    op1=ALU.add,
+                    accum_out=r_sum[:, k : k + 1],
                 )
-                neg_mean = norm.tile([P, 1], F32)
-                nc.gpsimd.tensor_scalar(
-                    out=neg_mean[:], in0=r_sum[:], scalar1=-1.0 / D, scalar2=0.0, op0=ALU.mult, op1=ALU.add
-                )
+                tiles["r", n, i] = r
+            neg_mean = norm.tile([P, TILES_PER_HALF], F32)
+            nc.vector.tensor_scalar(
+                out=neg_mean[:], in0=r_sum[:], scalar1=-1.0 / D, scalar2=0.0, op0=ALU.mult, op1=ALU.add
+            )
+            tiles["neg_mean", n, half] = neg_mean
+
+        def inverse_deviation(n, half):
+            sq_sum = norm.tile([P, TILES_PER_HALF], F32)
+            for k in range(TILES_PER_HALF):
                 squares = norm.tile([P, D], BF16)
-                sq_sum = norm.tile([P, 1], F32)
                 nc.scalar.activation(
-                    out=squares[:], in_=r[:], func=ACT.Square, bias=neg_mean[:], scale=1.0, accum_out=sq_sum[:]
+                    out=squares[:],
+                    in_=tiles["r", n, half * TILES_PER_HALF + k][:],
+                    func=ACT.Square,
+                    bias=tiles["neg_mean", n, half][:, k : k + 1],
+                    scale=1.0,
+                    accum_out=sq_sum[:, k : k + 1],
                 )
+            var_eps = norm.tile([P, TILES_PER_HALF], F32)
+            nc.gpsimd.tensor_scalar(
+                out=var_eps[:], in0=sq_sum[:], scalar1=1.0 / D, scalar2=LN_EPS, op0=ALU.mult, op1=ALU.add
+            )
+            rstd = norm.tile([P, TILES_PER_HALF], F32)
+            nc.gpsimd.tensor_tensor(out=rstd[:], in0=var_eps[:], in1=neg_half[:], op=ALU.pow)
+            tiles["rstd", n, half] = rstd
+
+        def centre_and_gain(n, half):
+            for k in range(TILES_PER_HALF):
+                i = half * TILES_PER_HALF + k
                 centred_gain = norm.tile([P, D], F32)
                 nc.vector.scalar_tensor_tensor(
-                    out=centred_gain[:], in0=r[:], scalar=neg_mean[:], in1=gain_bc[:], op0=ALU.add, op1=ALU.mult
+                    out=centred_gain[:],
+                    in0=tiles["r", n, i][:],
+                    scalar=tiles["neg_mean", n, half][:, k : k + 1],
+                    in1=tiles["gain", n][:],
+                    op0=ALU.add,
+                    op1=ALU.mult,
                 )
-                var_eps = norm.tile([P, 1], F32)
-                nc.gpsimd.tensor_scalar(
-                    out=var_eps[:], in0=sq_sum[:], scalar1=1.0 / D, scalar2=LN_EPS, op0=ALU.mult, op1=ALU.add
-                )
-                rstd = norm.tile([P, 1], F32)
-                nc.gpsimd.tensor_tensor(out=rstd[:], in0=var_eps[:], in1=neg_half[:], op=ALU.pow)
-                nc.vector.scalar_tensor_tensor(
-                    out=y[:, i, :], in0=centred_gain[:], scalar=rstd[:], in1=beta_bc[:], op0=ALU.mult, op1=ALU.add
-                )
-            for j in range(TASKS_PER_TILE):
-                nc.sync.dma_start(out=task_rows(out[:, n], j), in_=y[j:P:TASKS_PER_TILE, :, :])
+                tiles["centred_gain", n, i] = centred_gain
 
-        load(0)
-        load(1)
-        prepare(0)
+        def finish(n, half):
+            y = double.tile([P, TILES_PER_HALF, D], F32)
+            for k in range(TILES_PER_HALF):
+                nc.vector.scalar_tensor_tensor(
+                    out=y[:, k, :],
+                    in0=tiles["centred_gain", n, half * TILES_PER_HALF + k][:],
+                    scalar=tiles["rstd", n, half][:, k : k + 1],
+                    in1=tiles["beta", n][:],
+                    op0=ALU.mult,
+                    op1=ALU.add,
+                )
+            first = half * TILES_PER_HALF
+            for j in range(TASKS_PER_TILE):
+                nc.sync.dma_start(
+                    out=task_rows(out[:, n], j)[:, first : first + TILES_PER_HALF, :],
+                    in_=y[j:P:TASKS_PER_TILE, :, :],
+                )
+
+        add_task_embedding(0)
+        transpose_x(0, 0)
+        quantise_w1(0)
+        transpose_b1()
+        transpose_x(0, 1)
+        regroup_w2(0, 0)
+        quantise_x(0)
+        regroup_w2(0, 1)
+        residual_addend(0)
+
         for n in range(EXPERTS + 1):
+            second = n - 1 >= 0
+            first = n < EXPERTS
+            following = n + 1 < EXPERTS
             if n + 2 < EXPERTS:
                 load(n + 2)
-            if n >= 1:
-                second_layer(n - 1)
-            if n < EXPERTS:
-                first_layer(n)
-            if n + 1 < EXPERTS:
-                prepare(n + 1)
+            if following:
+                add_task_embedding(n + 1)
+            if first:
+                quantise_w2(n)
+                hidden_units(n, 0, 2)
+            if second:
+                second_product(n - 1, 0)
+            if first:
+                hidden_units(n, 2, 2)
+            if second:
+                second_product(n - 1, 1)
+            if first:
+                regroup_h(n, 0)
+            if second:
+                inverse_deviation(n - 1, 0)
+                inverse_deviation(n - 1, 1)
+                centre_and_gain(n - 1, 0)
+                centre_and_gain(n - 1, 1)
+            if first:
+                hidden_units(n, 4, 4)
+                quantise_h(n, 0)
+            if following:
+                quantise_w1(n + 1)
+            if first:
+                regroup_h(n, 1)
+            if second:
+                finish(n - 1, 0)
+                finish(n - 1, 1)
+            if following:
+                transpose_x(n + 1, 0)
+                regroup_w2(n + 1, 0)
+            if first:
+                quantise_h(n, 1)
+            if following:
+                transpose_x(n + 1, 1)
+                regroup_w2(n + 1, 1)
+                residual_addend(n + 1)
+                quantise_x(n + 1)

@@ -24,6 +24,7 @@ HALVES = 2
 TILES_PER_HALF = ROW_TILES // HALVES
 H_TILES = H // P
 H_PASSES = H // K_PASS
+D_CHUNKS = D // P
 LN_EPS = 1e-5
 
 FLOPS = 2 * EXPERTS * ROWS * (D * H + H * D)
@@ -41,19 +42,20 @@ def tile_hdmodel_pb_t_kernel(tc, xs_mix, task_emb, W1, b1, W2, b2, ln_g, ln_b, o
     with ExitStack() as ctx:
         const = ctx.enter_context(tc.tile_pool(name="const", bufs=1))
         loads = ctx.enter_context(tc.tile_pool(name="loads", bufs=2))
-        vectors = ctx.enter_context(tc.tile_pool(name="vectors", bufs=4))
         single = ctx.enter_context(tc.tile_pool(name="single", bufs=1))
         double = ctx.enter_context(tc.tile_pool(name="double", bufs=2))
+        triple = ctx.enter_context(tc.tile_pool(name="triple", bufs=3))
         norm = ctx.enter_context(tc.tile_pool(name="norm", bufs=ROW_TILES))
-        psum_t = ctx.enter_context(tc.psum_pool(name="psum_t", bufs=1))
-        psum_h = ctx.enter_context(tc.psum_pool(name="psum_h", bufs=3))
-        psum_o = ctx.enter_context(tc.psum_pool(name="psum_o", bufs=2))
-        psum_s = ctx.enter_context(tc.psum_pool(name="psum_s", bufs=2))
+        rows_pool = ctx.enter_context(tc.tile_pool(name="rows_pool", bufs=2 * ROW_TILES))
+        banks = ctx.enter_context(tc.psum_pool(name="banks", bufs=7))
+        psum_gb = ctx.enter_context(tc.psum_pool(name="psum_gb", bufs=1))
         ctx.enter_context(tc.manual_schedule())
 
         ident = const.tile([P, P], BF16)
         make_identity(nc, ident[:])
-        neg_half = const.tile([P, TILES_PER_HALF], F32)
+        ident_f32 = const.tile([P, P], F32)
+        nc.vector.tensor_copy(out=ident_f32[:], in_=ident[:])
+        neg_half = const.tile([P, ROW_TILES], F32)
         nc.vector.memset(neg_half[:], -0.5)
 
         def task_rows(dram_bpd, j):
@@ -73,20 +75,17 @@ def tile_hdmodel_pb_t_kernel(tc, xs_mix, task_emb, W1, b1, W2, b2, ln_g, ln_b, o
             for j in range(TASKS_PER_TILE):
                 nc.sync.dma_start(out=xm[j:P:TASKS_PER_TILE, :, :], in_=task_rows(xs_mix[:, n], j))
             w1_raw = loads.tile([P, PACK, H], BF16)
-            nc.sync.dma_start(out=w1_raw[:], in_=W1[n].rearrange("(t p) h -> p t h", p=P))
+            nc.sync.dma_start(
+                out=w1_raw[:].rearrange("p (u e) h -> p u e h", e=2),
+                in_=W1[n].rearrange("(u p e) h -> p u e h", u=2, e=2),
+            )
             w2_raw = loads.tile([P, H_PASSES, PACK, D], BF16)
             nc.sync.dma_start(
                 out=w2_raw[:], in_=W2[n].rearrange("(c t p) d -> p c t d", t=PACK, p=P)
             )
-            gain_bc = vectors.tile([P, D], BF16)
-            nc.sync.dma_start(out=gain_bc[:], in_=ln_g[n].partition_broadcast(P))
-            beta_bc = vectors.tile([P, D], BF16)
-            nc.sync.dma_start(out=beta_bc[:], in_=ln_b[n].partition_broadcast(P))
             tiles["xm", n] = xm
             tiles["w1_raw", n] = w1_raw
             tiles["w2_raw", n] = w2_raw
-            tiles["gain", n] = gain_bc
-            tiles["beta", n] = beta_bc
 
         load(0)
         load(1)
@@ -107,38 +106,55 @@ def tile_hdmodel_pb_t_kernel(tc, xs_mix, task_emb, W1, b1, W2, b2, ln_g, ln_b, o
         )
         nc.vector.memset(select[B2_ROW : B2_ROW + 1, :, :], 1.0)
 
-        b1_rows = const.tile([P, P], BF16)
-        nc.vector.memset(b1_rows[:], 0.0)
-        nc.scalar.dma_start(
-            out=b1_rows[0 : EXPERTS * H_TILES, :], in_=b1.rearrange("n (m q) -> (n m) q", q=P)
-        )
-        b1_cols = const.tile([P, EXPERTS * H_TILES], F32)
+        G_ROW = EXPERTS * H_TILES
+        B_ROW = G_ROW + EXPERTS * D_CHUNKS
+        vec_rows = const.tile([P, P], BF16)
+        nc.scalar.dma_start(out=vec_rows[0:G_ROW, :], in_=b1.rearrange("n (m q) -> (n m) q", q=P))
+        nc.scalar.dma_start(out=vec_rows[G_ROW:B_ROW, :], in_=ln_g.rearrange("n (m q) -> (n m) q", q=P))
+        nc.scalar.dma_start(out=vec_rows[B_ROW:P, :], in_=ln_b.rearrange("n (m q) -> (n m) q", q=P))
+        b1_cols = const.tile([P, G_ROW], F32)
+        gb_cols = const.tile([P, P - G_ROW], BF16)
 
-        def transpose_b1():
-            b1_t = psum_s.tile([P, P], BF16, tag="shift")
-            nc.tensor.transpose(b1_t[:], b1_rows[:], ident[:])
-            nc.vector.tensor_copy(out=b1_cols[:], in_=b1_t[:, 0 : EXPERTS * H_TILES])
+        def transpose_vectors():
+            vec_t = banks.tile([P, P], BF16, tag="bank")
+            nc.tensor.transpose(vec_t[:], vec_rows[:], ident[:])
+            nc.vector.tensor_copy(out=b1_cols[:], in_=vec_t[:, 0:G_ROW])
+            nc.vector.tensor_copy(out=gb_cols[:], in_=vec_t[:, G_ROW:P])
+
+        def spread_gain_beta(n):
+            gb = psum_gb.tile([P, 2, D], BF16)
+            for which in range(2):
+                for m in range(D_CHUNKS):
+                    col = which * EXPERTS * D_CHUNKS + n * D_CHUNKS + m
+                    nc.tensor.transpose(
+                        gb[:, which, m * P : (m + 1) * P],
+                        gb_cols[:, col : col + 1].to_broadcast([P, P]),
+                        ident[:],
+                    )
+            tiles["gb", n] = gb
 
         def add_task_embedding(n):
             xs_bf = double.tile([P, ROW_TILES, D], BF16)
             nc.vector.tensor_tensor(out=xs_bf[:], in0=tiles["xm", n][:], in1=te_rep[:], op=ALU.add)
-            x_grouped = double.tile([P, ROWS, PACK], BF16, align_bytes=64)
+            x_words = double.tile([P, ROWS, 2], F32, align_bytes=64)
             tiles["xs_bf", n] = xs_bf
-            tiles["x_grouped", n] = x_grouped
+            tiles["x_words", n] = x_words
 
         def transpose_x(n, half):
-            xt = psum_t.tile([P, TILES_PER_HALF, PACK, P], BF16, tag="xt")
+            xt = banks.tile([P, TILES_PER_HALF, 2, P], F32, tag="bank")
+            words = tiles["xs_bf", n][:].bitcast(F32)
             for i in range(TILES_PER_HALF):
-                for t in range(PACK):
+                for u in range(2):
                     nc.tensor.transpose(
-                        xt[:, i, t, :],
-                        tiles["xs_bf", n][:, half * TILES_PER_HALF + i, t * P : (t + 1) * P],
-                        ident[:],
+                        xt[:, i, u, :], words[:, half * TILES_PER_HALF + i, u * P : (u + 1) * P], ident_f32[:]
                     )
+            tiles["xt", n, half] = xt
+
+        def copy_x(n, half):
             rows = slice(half * TILES_PER_HALF * P, (half + 1) * TILES_PER_HALF * P)
             nc.scalar.copy(
-                out=tiles["x_grouped", n][:, rows, :].rearrange("p (i r) t -> p i r t", i=TILES_PER_HALF),
-                in_=xt[:].rearrange("p i t r -> p i r t"),
+                out=tiles["x_words", n][:, rows, :].rearrange("p (i r) u -> p i r u", i=TILES_PER_HALF),
+                in_=tiles["xt", n, half][:].rearrange("p i u r -> p i r u"),
             )
 
         def quantise_x(n):
@@ -147,54 +163,80 @@ def tile_hdmodel_pb_t_kernel(tc, xs_mix, task_emb, W1, b1, W2, b2, ln_g, ln_b, o
             nc.vector.quantize_mx(
                 out=x_codes[:].bitcast(FP8X4),
                 scales=x_scales[:],
-                in_=tiles["x_grouped", n][:].rearrange("p r t -> p (r t)"),
+                in_=tiles["x_words", n][:].rearrange("p r u -> p (r u)").bitcast(BF16),
             )
             tiles["x_codes", n] = x_codes
             tiles["x_scales", n] = x_scales
 
-        def quantise_w1(n):
+        def gpsimd_regroup(grouped, planes):
+            nc.gpsimd.tensor_scalar(
+                out=grouped,
+                in0=planes.rearrange("p t w -> p w t"),
+                scalar1=1.0,
+                scalar2=0.0,
+                op0=ALU.mult,
+                op1=ALU.add,
+            )
+
+        def new_grouped_weights(n):
             w1_grouped = single.tile([P, H, PACK], BF16, align_bytes=64)
+            w2_grouped = single.tile([P, H_PASSES, D, PACK], BF16, align_bytes=64)
+            tiles["w1_grouped", n] = w1_grouped
+            tiles["w2_grouped", n] = w2_grouped
+
+        def regroup_w1(n, engine, first, count):
+            cols = slice(first, first + count)
+            grouped = tiles["w1_grouped", n][:, cols, :]
+            planes = tiles["w1_raw", n][:, :, cols]
+            if engine == "gpsimd":
+                gpsimd_regroup(grouped, planes)
+            elif engine == "vector":
+                regroup(nc.vector.tensor_copy, grouped, planes)
+            else:
+                regroup(nc.scalar.copy, grouped, planes)
+
+        def regroup_w2(n, engine, c):
+            grouped = tiles["w2_grouped", n][:, c, :, :]
+            planes = tiles["w2_raw", n][:, c, :, :]
+            if engine == "gpsimd":
+                gpsimd_regroup(grouped, planes)
+            else:
+                regroup(nc.scalar.copy, grouped, planes)
+
+        def quantise_w1(n):
             w1_codes = double.tile([P, H], U32, align_bytes=64)
             w1_scales = double.tile([P, H], U8, align_bytes=64)
-            half_h = H // 2
-            for s in range(2):
-                cols = slice(s * half_h, (s + 1) * half_h)
-                regroup(nc.vector.tensor_copy, w1_grouped[:, cols, :], tiles["w1_raw", n][:, :, cols])
-            for s in range(2):
-                cols = slice(s * half_h, (s + 1) * half_h)
-                nc.vector.quantize_mx(
-                    out=w1_codes[:, cols].bitcast(FP8X4),
-                    scales=w1_scales[:, cols],
-                    in_=w1_grouped[:, cols, :].rearrange("p w t -> p (w t)"),
-                )
+            nc.vector.quantize_mx(
+                out=w1_codes[:].bitcast(FP8X4),
+                scales=w1_scales[:],
+                in_=tiles["w1_grouped", n][:].rearrange("p w t -> p (w t)"),
+            )
             tiles["w1_codes", n] = w1_codes
             tiles["w1_scales", n] = w1_scales
-
-        def regroup_w2(n, c):
-            if c == 0:
-                w2_grouped = single.tile([P, H_PASSES, D, PACK], BF16, align_bytes=64)
-                tiles["w2_grouped", n] = w2_grouped
-            regroup(nc.scalar.copy, tiles["w2_grouped", n][:, c, :, :], tiles["w2_raw", n][:, c, :, :])
 
         def quantise_w2(n):
             w2_codes = double.tile([P, H_PASSES, D], U32, align_bytes=64)
             w2_scales = double.tile([P, H_PASSES, D], U8, align_bytes=64)
-            for c in range(H_PASSES):
-                nc.vector.quantize_mx(
-                    out=w2_codes[:, c, :].bitcast(FP8X4),
-                    scales=w2_scales[:, c, :],
-                    in_=tiles["w2_grouped", n][:, c, :, :].rearrange("p w t -> p (w t)"),
-                )
+            nc.vector.quantize_mx(
+                out=w2_codes[:].rearrange("p c w -> p (c w)").bitcast(FP8X4),
+                scales=w2_scales[:].rearrange("p c w -> p (c w)"),
+                in_=tiles["w2_grouped", n][:].rearrange("p c w t -> p (c w t)"),
+            )
             tiles["w2_codes", n] = w2_codes
             tiles["w2_scales", n] = w2_scales
 
-        def residual_addend(n):
-            resid = double.tile([P, ROW_TILES, D], F32)
-            for i in range(ROW_TILES):
-                shift = psum_s.tile([P, D], F32)
-                nc.tensor.matmul(out=shift[:], lhsT=select[:, i, :], rhs=addends[:, n, :], start=True, stop=True)
-                nc.vector.tensor_tensor(out=resid[:, i, :], in0=shift[:], in1=tiles["xm", n][:, i, :], op=ALU.add)
-            tiles["resid", n] = resid
+        def shift_rows(n, i):
+            shift = banks.tile([P, D], F32, tag="bank")
+            nc.tensor.matmul(out=shift[:], lhsT=select[:, i, :], rhs=addends[:, n, :], start=True, stop=True)
+            tiles["shift", n, i] = shift
+
+        def residual_addend(n, i):
+            if i == 0:
+                resid = triple.tile([P, ROW_TILES, D], F32)
+                tiles["resid", n] = resid
+            nc.vector.tensor_tensor(
+                out=tiles["resid", n][:, i, :], in0=tiles["shift", n, i][:], in1=tiles["xm", n][:, i, :], op=ALU.add
+            )
 
         def hidden_units(n, first, count):
             if first == 0:
@@ -202,7 +244,7 @@ def tile_hdmodel_pb_t_kernel(tc, xs_mix, task_emb, W1, b1, W2, b2, ln_g, ln_b, o
                 tiles["h_t", n] = h_t
             for m in range(first, first + count):
                 units = slice(m * P, (m + 1) * P)
-                pre = psum_h.tile([P, ROWS], F32)
+                pre = banks.tile([P, ROWS], F32, tag="bank")
                 nc.tensor.matmul_mx(
                     out=pre[:],
                     lhsT=tiles["w1_codes", n][:, units].bitcast(FP8X4),
@@ -212,9 +254,17 @@ def tile_hdmodel_pb_t_kernel(tc, xs_mix, task_emb, W1, b1, W2, b2, ln_g, ln_b, o
                     start=True,
                     stop=True,
                 )
+                tiles["pre", n, m] = pre
+
+        def silu(n, first, count):
+            for m in range(first, first + count):
                 col = n * H_TILES + m
                 nc.scalar.activation(
-                    out=tiles["h_t", n][:, m, :], in_=pre[:], func=ACT.Silu, bias=b1_cols[:, col : col + 1], scale=1.0
+                    out=tiles["h_t", n][:, m, :],
+                    in_=tiles["pre", n, m][:],
+                    func=ACT.Silu,
+                    bias=b1_cols[:, col : col + 1],
+                    scale=1.0,
                 )
 
         def regroup_h(n, c):
@@ -234,142 +284,167 @@ def tile_hdmodel_pb_t_kernel(tc, xs_mix, task_emb, W1, b1, W2, b2, ln_g, ln_b, o
                 in_=tiles["h_grouped", n, c][:].rearrange("p r t -> p (r t)"),
             )
 
-        def second_product(n, half):
-            r_sum = norm.tile([P, TILES_PER_HALF], F32)
-            for k in range(TILES_PER_HALF):
-                i = half * TILES_PER_HALF + k
-                rows = slice(i * P, (i + 1) * P)
-                mlp = psum_o.tile([P, D], F32)
-                for c in range(H_PASSES):
-                    nc.tensor.matmul_mx(
-                        out=mlp[:],
-                        lhsT=tiles["h_codes", n][:, c, rows].bitcast(FP8X4),
-                        lhsT_scale=tiles["h_scales", n][:, c, rows],
-                        rhs=tiles["w2_codes", n][:, c, :].bitcast(FP8X4),
-                        rhs_scale=tiles["w2_scales", n][:, c, :],
-                        start=(c == 0),
-                        stop=(c == H_PASSES - 1),
-                    )
-                r = norm.tile([P, D], F32)
-                nc.vector.scalar_tensor_tensor(
-                    out=r[:],
-                    in0=mlp[:],
-                    scalar=1.0,
-                    in1=tiles["resid", n][:, i, :],
-                    op0=ALU.mult,
-                    op1=ALU.add,
-                    accum_out=r_sum[:, k : k + 1],
+        def second_product(n, i):
+            rows = slice(i * P, (i + 1) * P)
+            mlp = banks.tile([P, D], F32, tag="bank")
+            for c in range(H_PASSES):
+                nc.tensor.matmul_mx(
+                    out=mlp[:],
+                    lhsT=tiles["h_codes", n][:, c, rows].bitcast(FP8X4),
+                    lhsT_scale=tiles["h_scales", n][:, c, rows],
+                    rhs=tiles["w2_codes", n][:, c, :].bitcast(FP8X4),
+                    rhs_scale=tiles["w2_scales", n][:, c, :],
+                    start=(c == 0),
+                    stop=(c == H_PASSES - 1),
                 )
-                tiles["r", n, i] = r
-            neg_mean = norm.tile([P, TILES_PER_HALF], F32)
-            nc.vector.tensor_scalar(
-                out=neg_mean[:], in0=r_sum[:], scalar1=-1.0 / D, scalar2=0.0, op0=ALU.mult, op1=ALU.add
-            )
-            tiles["neg_mean", n, half] = neg_mean
+            tiles["mlp", n, i] = mlp
 
-        def inverse_deviation(n, half):
-            sq_sum = norm.tile([P, TILES_PER_HALF], F32)
-            for k in range(TILES_PER_HALF):
-                squares = norm.tile([P, D], BF16)
+        def residual_sum(n, i):
+            if i == 0:
+                r_sum = triple.tile([P, ROW_TILES], F32)
+                neg_mean = triple.tile([P, ROW_TILES], F32)
+                sq_sum = triple.tile([P, ROW_TILES], F32)
+                tiles["r_sum", n] = r_sum
+                tiles["neg_mean", n] = neg_mean
+                tiles["sq_sum", n] = sq_sum
+            r = rows_pool.tile([P, D], F32)
+            nc.vector.scalar_tensor_tensor(
+                out=r[:],
+                in0=tiles["mlp", n, i][:],
+                scalar=1.0,
+                in1=tiles["resid", n][:, i, :],
+                op0=ALU.mult,
+                op1=ALU.add,
+                accum_out=tiles["r_sum", n][:, i : i + 1],
+            )
+            tiles["r", n, i] = r
+
+        def squared_deviations(n, half):
+            cols = slice(half * TILES_PER_HALF, (half + 1) * TILES_PER_HALF)
+            nc.scalar.activation(
+                out=tiles["neg_mean", n][:, cols], in_=tiles["r_sum", n][:, cols], func=ACT.Copy, scale=-1.0 / D
+            )
+            for i in range(cols.start, cols.stop):
+                squares = double.tile([P, D], BF16)
                 nc.scalar.activation(
                     out=squares[:],
-                    in_=tiles["r", n, half * TILES_PER_HALF + k][:],
+                    in_=tiles["r", n, i][:],
                     func=ACT.Square,
-                    bias=tiles["neg_mean", n, half][:, k : k + 1],
+                    bias=tiles["neg_mean", n][:, i : i + 1],
                     scale=1.0,
-                    accum_out=sq_sum[:, k : k + 1],
+                    accum_out=tiles["sq_sum", n][:, i : i + 1],
                 )
-            var_eps = norm.tile([P, TILES_PER_HALF], F32)
-            nc.gpsimd.tensor_scalar(
-                out=var_eps[:], in0=sq_sum[:], scalar1=1.0 / D, scalar2=LN_EPS, op0=ALU.mult, op1=ALU.add
-            )
-            rstd = norm.tile([P, TILES_PER_HALF], F32)
-            nc.gpsimd.tensor_tensor(out=rstd[:], in0=var_eps[:], in1=neg_half[:], op=ALU.pow)
-            tiles["rstd", n, half] = rstd
 
-        def centre_and_gain(n, half):
-            for k in range(TILES_PER_HALF):
-                i = half * TILES_PER_HALF + k
-                centred_gain = norm.tile([P, D], F32)
-                nc.vector.scalar_tensor_tensor(
-                    out=centred_gain[:],
-                    in0=tiles["r", n, i][:],
-                    scalar=tiles["neg_mean", n, half][:, k : k + 1],
-                    in1=tiles["gain", n][:],
-                    op0=ALU.add,
-                    op1=ALU.mult,
-                )
-                tiles["centred_gain", n, i] = centred_gain
+        def inverse_deviation(n):
+            var_eps = triple.tile([P, ROW_TILES], F32)
+            nc.gpsimd.tensor_scalar(
+                out=var_eps[:], in0=tiles["sq_sum", n][:], scalar1=1.0 / D, scalar2=LN_EPS, op0=ALU.mult, op1=ALU.add
+            )
+            rstd = triple.tile([P, ROW_TILES], F32)
+            nc.gpsimd.tensor_tensor(out=rstd[:], in0=var_eps[:], in1=neg_half[:], op=ALU.pow)
+            tiles["rstd", n] = rstd
+
+        def centre_and_gain(n, i):
+            centred_gain = norm.tile([P, D], F32)
+            nc.vector.scalar_tensor_tensor(
+                out=centred_gain[:],
+                in0=tiles["r", n, i][:],
+                scalar=tiles["neg_mean", n][:, i : i + 1],
+                in1=tiles["gb", n][:, 0, :],
+                op0=ALU.add,
+                op1=ALU.mult,
+            )
+            tiles["centred_gain", n, i] = centred_gain
 
         def finish(n, half):
             y = double.tile([P, TILES_PER_HALF, D], F32)
+            first = half * TILES_PER_HALF
             for k in range(TILES_PER_HALF):
                 nc.vector.scalar_tensor_tensor(
                     out=y[:, k, :],
-                    in0=tiles["centred_gain", n, half * TILES_PER_HALF + k][:],
-                    scalar=tiles["rstd", n, half][:, k : k + 1],
-                    in1=tiles["beta", n][:],
+                    in0=tiles["centred_gain", n, first + k][:],
+                    scalar=tiles["rstd", n][:, first + k : first + k + 1],
+                    in1=tiles["gb", n][:, 1, :],
                     op0=ALU.mult,
                     op1=ALU.add,
                 )
-            first = half * TILES_PER_HALF
             for j in range(TASKS_PER_TILE):
                 nc.sync.dma_start(
                     out=task_rows(out[:, n], j)[:, first : first + TILES_PER_HALF, :],
                     in_=y[j:P:TASKS_PER_TILE, :, :],
                 )
 
-        add_task_embedding(0)
-        transpose_x(0, 0)
-        quantise_w1(0)
-        transpose_b1()
-        transpose_x(0, 1)
-        regroup_w2(0, 0)
-        quantise_x(0)
-        regroup_w2(0, 1)
-        residual_addend(0)
+        def is_expert(n):
+            return 0 <= n < EXPERTS
 
-        for n in range(EXPERTS + 1):
-            second = n - 1 >= 0
-            first = n < EXPERTS
-            following = n + 1 < EXPERTS
-            if n + 2 < EXPERTS:
-                load(n + 2)
-            if following:
-                add_task_embedding(n + 1)
-            if first:
-                quantise_w2(n)
-                hidden_units(n, 0, 2)
-            if second:
-                second_product(n - 1, 0)
-            if first:
-                hidden_units(n, 2, 2)
-            if second:
-                second_product(n - 1, 1)
-            if first:
-                regroup_h(n, 0)
-            if second:
-                inverse_deviation(n - 1, 0)
-                inverse_deviation(n - 1, 1)
-                centre_and_gain(n - 1, 0)
-                centre_and_gain(n - 1, 1)
-            if first:
-                hidden_units(n, 4, 4)
-                quantise_h(n, 0)
-            if following:
-                quantise_w1(n + 1)
-            if first:
-                regroup_h(n, 1)
-            if second:
-                finish(n - 1, 0)
-                finish(n - 1, 1)
-            if following:
-                transpose_x(n + 1, 0)
-                regroup_w2(n + 1, 0)
-            if first:
-                quantise_h(n, 1)
-            if following:
-                transpose_x(n + 1, 1)
-                regroup_w2(n + 1, 1)
-                residual_addend(n + 1)
-                quantise_x(n + 1)
+        for r in range(-1, EXPERTS + 2):
+            following, this, before, last = r + 1, r, r - 1, r - 2
+            if r >= 0 and is_expert(r + 2):
+                load(r + 2)
+            if is_expert(this):
+                quantise_x(this)
+                quantise_w1(this)
+                hidden_units(this, 0, 4)
+            if is_expert(before):
+                quantise_h(before, 0)
+                quantise_h(before, 1)
+                second_product(before, 0)
+                second_product(before, 1)
+            if is_expert(this):
+                hidden_units(this, 4, 4)
+                silu(this, 0, H_TILES)
+            if is_expert(following):
+                add_task_embedding(following)
+            if is_expert(this):
+                quantise_w2(this)
+            if is_expert(following):
+                new_grouped_weights(following)
+                if following == 0:
+                    regroup_w1(following, "vector", 0, H // 2)
+                    regroup_w1(following, "vector", H // 2, H // 2)
+                    transpose_vectors()
+                else:
+                    regroup_w2(following, "gpsimd", 0)
+                    regroup_w1(following, "gpsimd", 0, H // 2)
+                    regroup_w1(following, "gpsimd", H // 2, H // 2)
+                shift_rows(following, 0)
+                shift_rows(following, 1)
+            if is_expert(before):
+                residual_sum(before, 0)
+                residual_sum(before, 1)
+                second_product(before, 2)
+                second_product(before, 3)
+            if is_expert(following):
+                residual_addend(following, 0)
+                residual_addend(following, 1)
+                shift_rows(following, 2)
+                shift_rows(following, 3)
+                transpose_x(following, 0)
+                transpose_x(following, 1)
+            if is_expert(this):
+                regroup_h(this, 0)
+            if is_expert(before):
+                residual_sum(before, 2)
+                residual_sum(before, 3)
+            if is_expert(following):
+                residual_addend(following, 2)
+                residual_addend(following, 3)
+                copy_x(following, 0)
+                copy_x(following, 1)
+            if is_expert(before):
+                squared_deviations(before, 0)
+                squared_deviations(before, 1)
+                inverse_deviation(before)
+            if is_expert(this):
+                regroup_h(this, 1)
+            if is_expert(following):
+                if following == 0:
+                    regroup_w2(following, "scalar", 0)
+                regroup_w2(following, "scalar", 1)
+            if is_expert(last):
+                for i in range(ROW_TILES):
+                    centre_and_gain(last, i)
+                finish(last, 0)
+                finish(last, 1)
+            if is_expert(before):
+                spread_gain_beta(before)

@@ -26,6 +26,7 @@ H_TILES = H // P
 H_PASSES = H // K_PASS
 D_CHUNKS = D // P
 LN_EPS = 1e-5
+W2_COLS_GPSIMD = 128
 
 FLOPS = 2 * EXPERTS * ROWS * (D * H + H * D)
 
@@ -51,6 +52,8 @@ def tile_hdmodel_pb_t_kernel(tc, xs_mix, task_emb, W1, b1, W2, b2, ln_g, ln_b, o
         psum_gb = ctx.enter_context(tc.psum_pool(name="psum_gb", bufs=1))
         ctx.enter_context(tc.manual_schedule())
 
+        addends = const.tile([P, EXPERTS, D], BF16)
+        nc.vector.memset(addends[:], 0.0)
         ident = const.tile([P, P], BF16)
         make_identity(nc, ident[:])
         ident_f32 = const.tile([P, P], F32)
@@ -70,28 +73,46 @@ def tile_hdmodel_pb_t_kernel(tc, xs_mix, task_emb, W1, b1, W2, b2, ln_g, ln_b, o
 
         tiles = {}
 
-        def load(n):
+        def load_x(n):
             xm = loads.tile([P, ROW_TILES, D], BF16)
             for j in range(TASKS_PER_TILE):
                 nc.sync.dma_start(out=xm[j:P:TASKS_PER_TILE, :, :], in_=task_rows(xs_mix[:, n], j))
+            tiles["xm", n] = xm
+
+        def load_w1(n, pieces):
             w1_raw = loads.tile([P, PACK, H], BF16)
-            nc.sync.dma_start(
-                out=w1_raw[:].rearrange("p (u e) h -> p u e h", e=2),
-                in_=W1[n].rearrange("(u p e) h -> p u e h", u=2, e=2),
-            )
+            tiles["w1_raw", n] = w1_raw
+            if pieces == 1:
+                nc.sync.dma_start(
+                    out=w1_raw[:].rearrange("p (u e) h -> p u e h", e=2),
+                    in_=W1[n].rearrange("(u p e) h -> p u e h", u=2, e=2),
+                )
+            else:
+                for s in range(pieces):
+                    cols = slice(s * (H // pieces), (s + 1) * (H // pieces))
+                    for u in range(2):
+                        nc.sync.dma_start(
+                            out=w1_raw[:, 2 * u : 2 * u + 2, cols],
+                            in_=W1[n, 2 * P * u : 2 * P * (u + 1), cols].rearrange("(p e) h -> p e h", e=2),
+                        )
+
+        def load_w2(n):
             w2_raw = loads.tile([P, H_PASSES, PACK, D], BF16)
             nc.sync.dma_start(
                 out=w2_raw[:], in_=W2[n].rearrange("(c t p) d -> p c t d", t=PACK, p=P)
             )
-            tiles["xm", n] = xm
-            tiles["w1_raw", n] = w1_raw
             tiles["w2_raw", n] = w2_raw
 
-        load(0)
+        def load(n):
+            load_x(n)
+            load_w1(n, 1)
+            load_w2(n)
+
+        load_x(0)
+        load_w1(0, 2)
+        load_w2(0)
         load(1)
 
-        addends = const.tile([P, EXPERTS, D], BF16)
-        nc.vector.memset(addends[:], 0.0)
         nc.scalar.dma_start(
             out=addends[0:TASKS, :, :], in_=task_emb.unsqueeze(1).to_broadcast([TASKS, EXPERTS, D])
         )
@@ -122,7 +143,10 @@ def tile_hdmodel_pb_t_kernel(tc, xs_mix, task_emb, W1, b1, W2, b2, ln_g, ln_b, o
             nc.vector.tensor_copy(out=gb_cols[:], in_=vec_t[:, G_ROW:P])
 
         def spread_gain_beta(n):
-            gb = psum_gb.tile([P, 2, D], BF16)
+            if n == EXPERTS - 1:
+                gb = banks.tile([P, 2, D], BF16, tag="bank")
+            else:
+                gb = psum_gb.tile([P, 2, D], BF16)
             for which in range(2):
                 for m in range(D_CHUNKS):
                     col = which * EXPERTS * D_CHUNKS + n * D_CHUNKS + m
@@ -195,11 +219,14 @@ def tile_hdmodel_pb_t_kernel(tc, xs_mix, task_emb, W1, b1, W2, b2, ln_g, ln_b, o
             else:
                 regroup(nc.scalar.copy, grouped, planes)
 
-        def regroup_w2(n, engine, c):
-            grouped = tiles["w2_grouped", n][:, c, :, :]
-            planes = tiles["w2_raw", n][:, c, :, :]
+        def regroup_w2(n, engine, c, first=0, count=D):
+            cols = slice(first, first + count)
+            grouped = tiles["w2_grouped", n][:, c, cols, :]
+            planes = tiles["w2_raw", n][:, c, :, cols]
             if engine == "gpsimd":
                 gpsimd_regroup(grouped, planes)
+            elif engine == "vector":
+                regroup(nc.vector.tensor_copy, grouped, planes)
             else:
                 regroup(nc.scalar.copy, grouped, planes)
 
@@ -267,9 +294,13 @@ def tile_hdmodel_pb_t_kernel(tc, xs_mix, task_emb, W1, b1, W2, b2, ln_g, ln_b, o
                     scale=1.0,
                 )
 
-        def regroup_h(n, c):
+        def regroup_h(n, engine, c):
             h_grouped = double.tile([P, ROWS, PACK], BF16, align_bytes=64)
-            regroup(nc.scalar.copy, h_grouped[:], tiles["h_t", n][:, c * PACK : (c + 1) * PACK, :])
+            planes = tiles["h_t", n][:, c * PACK : (c + 1) * PACK, :]
+            if engine == "gpsimd":
+                gpsimd_regroup(h_grouped[:], planes)
+            else:
+                regroup(nc.scalar.copy, h_grouped[:], planes)
             tiles["h_grouped", n, c] = h_grouped
 
         def quantise_h(n, c):
@@ -377,9 +408,20 @@ def tile_hdmodel_pb_t_kernel(tc, xs_mix, task_emb, W1, b1, W2, b2, ln_g, ln_b, o
         def is_expert(n):
             return 0 <= n < EXPERTS
 
-        for r in range(-1, EXPERTS + 2):
+        add_task_embedding(0)
+        transpose_x(0, 0)
+        transpose_x(0, 1)
+        new_grouped_weights(0)
+        regroup_w1(0, "vector", 0, H // 2)
+        copy_x(0, 0)
+        copy_x(0, 1)
+        regroup_w1(0, "vector", H // 2, H // 2)
+        transpose_vectors()
+
+        for r in range(EXPERTS + 2):
             following, this, before, last = r + 1, r, r - 1, r - 2
-            if r >= 0 and is_expert(r + 2):
+            vector_halves = max(0, 2 - r)
+            if is_expert(r + 2):
                 load(r + 2)
             if is_expert(this):
                 quantise_x(this)
@@ -390,25 +432,34 @@ def tile_hdmodel_pb_t_kernel(tc, xs_mix, task_emb, W1, b1, W2, b2, ln_g, ln_b, o
                 quantise_h(before, 1)
                 second_product(before, 0)
                 second_product(before, 1)
+            if following >= 2 and is_expert(following):
+                shift_rows(following, 0)
+                shift_rows(following, 1)
             if is_expert(this):
                 hidden_units(this, 4, 4)
                 silu(this, 0, H_TILES)
             if is_expert(following):
                 add_task_embedding(following)
+            if this == 0:
+                regroup_w2(this, "vector", 0)
+                regroup_w2(this, "vector", 1)
             if is_expert(this):
                 quantise_w2(this)
             if is_expert(following):
                 new_grouped_weights(following)
-                if following == 0:
-                    regroup_w1(following, "vector", 0, H // 2)
-                    regroup_w1(following, "vector", H // 2, H // 2)
-                    transpose_vectors()
-                else:
-                    regroup_w2(following, "gpsimd", 0)
-                    regroup_w1(following, "gpsimd", 0, H // 2)
-                    regroup_w1(following, "gpsimd", H // 2, H // 2)
+                regroup_w2(following, "gpsimd", 0)
+                for s in range(2 - vector_halves):
+                    regroup_w1(following, "gpsimd", s * (H // 2), H // 2)
+                regroup_w2(following, "gpsimd", 1, 0, W2_COLS_GPSIMD)
+            if this == 0:
+                for i in range(ROW_TILES):
+                    shift_rows(this, i)
+                    residual_addend(this, i)
                 shift_rows(following, 0)
                 shift_rows(following, 1)
+            if is_expert(last) and not is_expert(this):
+                for i in range(ROW_TILES):
+                    centre_and_gain(last, i)
             if is_expert(before):
                 residual_sum(before, 0)
                 residual_sum(before, 1)
@@ -422,29 +473,33 @@ def tile_hdmodel_pb_t_kernel(tc, xs_mix, task_emb, W1, b1, W2, b2, ln_g, ln_b, o
                 transpose_x(following, 0)
                 transpose_x(following, 1)
             if is_expert(this):
-                regroup_h(this, 0)
+                regroup_h(this, "scalar", 0)
+                if not is_expert(following):
+                    regroup_h(this, "gpsimd", 1)
             if is_expert(before):
                 residual_sum(before, 2)
                 residual_sum(before, 3)
+            if before == EXPERTS - 1:
+                spread_gain_beta(before)
             if is_expert(following):
                 residual_addend(following, 2)
                 residual_addend(following, 3)
-                copy_x(following, 0)
-                copy_x(following, 1)
+                for s in range(2 - vector_halves, 2):
+                    regroup_w1(following, "vector", s * (H // 2), H // 2)
             if is_expert(before):
                 squared_deviations(before, 0)
                 squared_deviations(before, 1)
                 inverse_deviation(before)
-            if is_expert(this):
-                regroup_h(this, 1)
             if is_expert(following):
-                if following == 0:
-                    regroup_w2(following, "scalar", 0)
-                regroup_w2(following, "scalar", 1)
+                copy_x(following, 0)
+                copy_x(following, 1)
+                regroup_h(this, "scalar", 1)
+                regroup_w2(following, "scalar", 1, W2_COLS_GPSIMD, D - W2_COLS_GPSIMD)
             if is_expert(last):
-                for i in range(ROW_TILES):
-                    centre_and_gain(last, i)
+                if is_expert(this):
+                    for i in range(ROW_TILES):
+                        centre_and_gain(last, i)
                 finish(last, 0)
                 finish(last, 1)
-            if is_expert(before):
+            if is_expert(before) and before < EXPERTS - 1:
                 spread_gain_beta(before)

@@ -105,13 +105,15 @@ def tile_hdmodel_pb_t_kernel(tc, xs_mix, task_emb, W1, b1, W2, b2, ln_g, ln_b, o
 
         def load(n):
             load_x(n)
-            load_w1(n, 1)
             load_w2(n)
+            load_w1(n, 1)
 
         load_x(0)
         load_w1(0, 2)
+        load_x(1)
         load_w2(0)
-        load(1)
+        load_w2(1)
+        load_w1(1, 1)
 
         nc.scalar.dma_start(
             out=addends[0:TASKS, :, :], in_=task_emb.unsqueeze(1).to_broadcast([TASKS, EXPERTS, D])

@@ -44,6 +44,7 @@ def tile_hdmodel_pb_t_kernel(tc, xs_mix, task_emb, W1, b1, W2, b2, ln_g, ln_b, o
         const = ctx.enter_context(tc.tile_pool(name="const", bufs=1))
         loads = ctx.enter_context(tc.tile_pool(name="loads", bufs=2))
         single = ctx.enter_context(tc.tile_pool(name="single", bufs=1))
+        x_loads = ctx.enter_context(tc.tile_pool(name="x_loads", bufs=3))
         double = ctx.enter_context(tc.tile_pool(name="double", bufs=2))
         triple = ctx.enter_context(tc.tile_pool(name="triple", bufs=3))
         norm = ctx.enter_context(tc.tile_pool(name="norm", bufs=ROW_TILES))
@@ -74,7 +75,7 @@ def tile_hdmodel_pb_t_kernel(tc, xs_mix, task_emb, W1, b1, W2, b2, ln_g, ln_b, o
         tiles = {}
 
         def load_x(n):
-            xm = loads.tile([P, ROW_TILES, D], BF16)
+            xm = x_loads.tile([P, ROW_TILES, D], BF16)
             for j in range(TASKS_PER_TILE):
                 nc.sync.dma_start(out=xm[j:P:TASKS_PER_TILE, :, :], in_=task_rows(xs_mix[:, n], j))
             tiles["xm", n] = xm
@@ -259,10 +260,11 @@ def tile_hdmodel_pb_t_kernel(tc, xs_mix, task_emb, W1, b1, W2, b2, ln_g, ln_b, o
             nc.tensor.matmul(out=shift[:], lhsT=select[:, i, :], rhs=addends[:, n, :], start=True, stop=True)
             tiles["shift", n, i] = shift
 
+        def new_residual_addend(n):
+            resid = triple.tile([P, ROW_TILES, D], F32)
+            tiles["resid", n] = resid
+
         def residual_addend(n, i):
-            if i == 0:
-                resid = triple.tile([P, ROW_TILES, D], F32)
-                tiles["resid", n] = resid
             nc.vector.tensor_tensor(
                 out=tiles["resid", n][:, i, :], in0=tiles["shift", n, i][:], in1=tiles["xm", n][:, i, :], op=ALU.add
             )
@@ -389,10 +391,16 @@ def tile_hdmodel_pb_t_kernel(tc, xs_mix, task_emb, W1, b1, W2, b2, ln_g, ln_b, o
             )
             tiles["centred_gain", n, i] = centred_gain
 
-        def finish(n, half):
-            y = double.tile([P, TILES_PER_HALF, D], F32)
-            first = half * TILES_PER_HALF
-            for k in range(TILES_PER_HALF):
+        def store_rows(n, first, count, y):
+            for j in range(TASKS_PER_TILE):
+                nc.sync.dma_start(
+                    out=task_rows(out[:, n], j)[:, first : first + count, :],
+                    in_=y[j:P:TASKS_PER_TILE, :, :],
+                )
+
+        def finish(n, first, count):
+            y = norm.tile([P, TILES_PER_HALF, D], F32)
+            for k in range(count):
                 nc.vector.scalar_tensor_tensor(
                     out=y[:, k, :],
                     in0=tiles["centred_gain", n, first + k][:],
@@ -401,14 +409,38 @@ def tile_hdmodel_pb_t_kernel(tc, xs_mix, task_emb, W1, b1, W2, b2, ln_g, ln_b, o
                     op0=ALU.mult,
                     op1=ALU.add,
                 )
-            for j in range(TASKS_PER_TILE):
-                nc.sync.dma_start(
-                    out=task_rows(out[:, n], j)[:, first : first + TILES_PER_HALF, :],
-                    in_=y[j:P:TASKS_PER_TILE, :, :],
-                )
+            store_rows(n, first, count, y[:, 0:count, :])
+
+        def load_gain_beta(n):
+            gain_sb = triple.tile([P, D], BF16)
+            nc.sync.dma_start(out=gain_sb[:], in_=ln_g[n].partition_broadcast(P))
+            beta_sb = triple.tile([P, D], BF16)
+            nc.sync.dma_start(out=beta_sb[:], in_=ln_b[n].partition_broadcast(P))
+            tiles["gain_sb", n] = gain_sb
+            tiles["beta_sb", n] = beta_sb
+
+        def gpsimd_finish(n, i):
+            scratch = single.tile([P, 2, D], F32, tag="w2_grouped", align_bytes=64)
+            z = scratch[:, 0, :]
+            z_gain = scratch[:, 1, :]
+            nc.gpsimd.tensor_scalar(
+                out=z,
+                in0=tiles["r", n, i][:],
+                scalar1=tiles["neg_mean", n][:, i : i + 1],
+                scalar2=tiles["rstd", n][:, i : i + 1],
+                op0=ALU.add,
+                op1=ALU.mult,
+            )
+            nc.gpsimd.tensor_tensor(out=z_gain, in0=z, in1=tiles["gain_sb", n][:], op=ALU.mult)
+            y_one = double.tile([P, 1, D], F32)
+            nc.gpsimd.tensor_tensor(out=y_one[:, 0, :], in0=z_gain, in1=tiles["beta_sb", n][:], op=ALU.add)
+            store_rows(n, i, 1, y_one[:])
 
         def is_expert(n):
             return 0 <= n < EXPERTS
+
+        def gpsimd_finishes(n):
+            return is_expert(n) and not is_expert(n + 3) and is_expert(n + 1)
 
         add_task_embedding(0)
         transpose_x(0, 0)
@@ -423,8 +455,12 @@ def tile_hdmodel_pb_t_kernel(tc, xs_mix, task_emb, W1, b1, W2, b2, ln_g, ln_b, o
         for r in range(EXPERTS + 2):
             following, this, before, last = r + 1, r, r - 1, r - 2
             vector_halves = max(0, 2 - r)
+            gpsimd_tiles = 1 if gpsimd_finishes(last) else 0
+            vector_tiles = ROW_TILES - gpsimd_tiles
             if is_expert(r + 2):
                 load(r + 2)
+            if gpsimd_finishes(this):
+                load_gain_beta(this)
             if is_expert(this):
                 quantise_x(this)
                 quantise_w1(this)
@@ -432,9 +468,10 @@ def tile_hdmodel_pb_t_kernel(tc, xs_mix, task_emb, W1, b1, W2, b2, ln_g, ln_b, o
             if is_expert(before):
                 quantise_h(before, 0)
                 quantise_h(before, 1)
+            if before >= 1 and is_expert(before):
                 second_product(before, 0)
                 second_product(before, 1)
-            if following >= 2 and is_expert(following):
+            if following >= 3 and is_expert(following):
                 shift_rows(following, 0)
                 shift_rows(following, 1)
             if is_expert(this):
@@ -453,14 +490,23 @@ def tile_hdmodel_pb_t_kernel(tc, xs_mix, task_emb, W1, b1, W2, b2, ln_g, ln_b, o
                 for s in range(2 - vector_halves):
                     regroup_w1(following, "gpsimd", s * (H // 2), H // 2)
                 regroup_w2(following, "gpsimd", 1, 0, W2_COLS_GPSIMD)
+            if gpsimd_tiles >= 1:
+                gpsimd_finish(last, ROW_TILES - 1)
             if this == 0:
+                new_residual_addend(this)
+                shift_rows(following, 0)
+                shift_rows(following, 1)
+
+            if before == 0:
                 for i in range(ROW_TILES):
-                    shift_rows(this, i)
-                    residual_addend(this, i)
+                    shift_rows(before, i)
+                    residual_addend(before, i)
+                second_product(before, 0)
+                second_product(before, 1)
                 shift_rows(following, 0)
                 shift_rows(following, 1)
             if is_expert(last) and not is_expert(this):
-                for i in range(ROW_TILES):
+                for i in range(vector_tiles):
                     centre_and_gain(last, i)
             if is_expert(before):
                 residual_sum(before, 0)
@@ -468,6 +514,7 @@ def tile_hdmodel_pb_t_kernel(tc, xs_mix, task_emb, W1, b1, W2, b2, ln_g, ln_b, o
                 second_product(before, 2)
                 second_product(before, 3)
             if is_expert(following):
+                new_residual_addend(following)
                 residual_addend(following, 0)
                 residual_addend(following, 1)
                 shift_rows(following, 2)
@@ -499,9 +546,9 @@ def tile_hdmodel_pb_t_kernel(tc, xs_mix, task_emb, W1, b1, W2, b2, ln_g, ln_b, o
                 regroup_w2(following, "scalar", 1, W2_COLS_GPSIMD, D - W2_COLS_GPSIMD)
             if is_expert(last):
                 if is_expert(this):
-                    for i in range(ROW_TILES):
+                    for i in range(vector_tiles):
                         centre_and_gain(last, i)
-                finish(last, 0)
-                finish(last, 1)
+                finish(last, 0, TILES_PER_HALF)
+                finish(last, TILES_PER_HALF, vector_tiles - TILES_PER_HALF)
             if is_expert(before) and before < EXPERTS - 1:
                 spread_gain_beta(before)

@@ -197,8 +197,8 @@ def tile_hdmodel_pb_t_kernel(tc, xs_mix, task_emb, W1, b1, W2, b2, ln_g, ln_b, o
 
         def gpsimd_regroup(grouped, planes):
             nc.gpsimd.tensor_scalar(
-                out=grouped,
-                in0=planes.rearrange("p t w -> p w t"),
+                out=grouped.rearrange("p (c i) t -> p c t i", i=4),
+                in0=planes.rearrange("p t (c i) -> p c t i", i=4),
                 scalar1=1.0,
                 scalar2=0.0,
                 op0=ALU.mult,

from contextlib import ExitStack

import concourse.mybir as mybir
from concourse.masks import make_identity

F32 = mybir.dt.float32
BF16 = mybir.dt.bfloat16
U32 = mybir.dt.uint32
U8 = mybir.dt.uint8
FP8X4 = mybir.dt.float8_e4m3fn_x4
ALU = mybir.AluOpType
ACT = mybir.ActivationFunctionType

P = 128
PACK = 4
K_PASS = P * PACK

BATCH, EXPERTS, TASKS, D, H = 32, 8, 16, 512, 1024
ROWS = BATCH * TASKS
ROW_TILES = ROWS // P
TASKS_PER_TILE = P // BATCH
B2_ROW = 32
HALVES = 2
TILES_PER_HALF = ROW_TILES // HALVES
H_TILES = H // P
H_PASSES = H // K_PASS
D_CHUNKS = D // P
LN_EPS = 1e-5
W2_COLS_GPSIMD = 128

FLOPS = 2 * EXPERTS * ROWS * (D * H + H * D)


def regroup(copy, grouped, planes):
    copy(
        out=grouped.rearrange("p (c i) t -> p c t i", i=4),
        in_=planes.rearrange("p t (c i) -> p c t i", i=4),
    )


def tile_hdmodel_pb_t_kernel(tc, xs_mix, task_emb, W1, b1, W2, b2, ln_g, ln_b, out):
    nc = tc.nc
    with ExitStack() as ctx:
        const = ctx.enter_context(tc.tile_pool(name="const", bufs=1))
        loads = ctx.enter_context(tc.tile_pool(name="loads", bufs=2))
        single = ctx.enter_context(tc.tile_pool(name="single", bufs=1))
        x_loads = ctx.enter_context(tc.tile_pool(name="x_loads", bufs=3))
        double = ctx.enter_context(tc.tile_pool(name="double", bufs=2))
        triple = ctx.enter_context(tc.tile_pool(name="triple", bufs=3))
        norm = ctx.enter_context(tc.tile_pool(name="norm", bufs=ROW_TILES))
        rows_pool = ctx.enter_context(tc.tile_pool(name="rows_pool", bufs=2 * ROW_TILES))
        banks = ctx.enter_context(tc.psum_pool(name="banks", bufs=7))
        psum_gb = ctx.enter_context(tc.psum_pool(name="psum_gb", bufs=1))
        ctx.enter_context(tc.manual_schedule())

        addends = const.tile([P, EXPERTS, D], BF16)
        nc.vector.memset(addends[:], 0.0)
        ident = const.tile([P, P], BF16)
        make_identity(nc, ident[:])
        ident_f32 = const.tile([P, P], F32)
        nc.vector.tensor_copy(out=ident_f32[:], in_=ident[:])
        neg_half = const.tile([P, ROW_TILES], F32)
        nc.vector.memset(neg_half[:], -0.5)

        def task_rows(dram_bpd, j):
            return dram_bpd.rearrange("b (i j) d -> j b i d", j=TASKS_PER_TILE)[j]

        te_rep = const.tile([P, ROW_TILES, D], BF16)
        for j in range(TASKS_PER_TILE):
            nc.scalar.dma_start(
                out=te_rep[j:P:TASKS_PER_TILE, :, :],
                in_=task_rows(task_emb.unsqueeze(0).to_broadcast([BATCH, TASKS, D]), j),
            )

        tiles = {}

        def load_x(n):
            xm = x_loads.tile([P, ROW_TILES, D], BF16)
            for j in range(TASKS_PER_TILE):
                nc.sync.dma_start(out=xm[j:P:TASKS_PER_TILE, :, :], in_=task_rows(xs_mix[:, n], j))
            tiles["xm", n] = xm

        def load_w1(n, pieces):
            w1_raw = loads.tile([P, PACK, H], BF16)
            tiles["w1_raw", n] = w1_raw
            if pieces == 1:
                nc.sync.dma_start(
                    out=w1_raw[:].rearrange("p (u e) h -> p u e h", e=2),
                    in_=W1[n].rearrange("(u p e) h -> p u e h", u=2, e=2),
                )
            else:
                for s in range(pieces):
                    cols = slice(s * (H // pieces), (s + 1) * (H // pieces))
                    for u in range(2):
                        nc.sync.dma_start(
                            out=w1_raw[:, 2 * u : 2 * u + 2, cols],
                            in_=W1[n, 2 * P * u : 2 * P * (u + 1), cols].rearrange("(p e) h -> p e h", e=2),
                        )

        def load_w2(n):
            w2_raw = loads.tile([P, H_PASSES, PACK, D], BF16)
            nc.sync.dma_start(
                out=w2_raw[:], in_=W2[n].rearrange("(c t p) d -> p c t d", t=PACK, p=P)
            )
            tiles["w2_raw", n] = w2_raw

        def load(n):
            load_x(n)
            load_w2(n)
            load_w1(n, 1)

        load_x(0)
        load_w1(0, 2)
        load_x(1)
        load_w2(0)
        load_w2(1)
        load_w1(1, 1)

        nc.scalar.dma_start(
            out=addends[0:TASKS, :, :], in_=task_emb.unsqueeze(1).to_broadcast([TASKS, EXPERTS, D])
        )
        nc.scalar.dma_start(out=addends[B2_ROW : B2_ROW + 1, :, :], in_=b2.unsqueeze(0))
        select = const.tile([P, ROW_TILES, P], BF16)
        nc.vector.tensor_copy(
            out=select[:].rearrange("k i (b j) -> k i b j", j=TASKS_PER_TILE),
            in_=ident[:, 0:TASKS]
            .rearrange("k (i j) -> k i j", j=TASKS_PER_TILE)
            .unsqueeze(2)
            .to_broadcast([P, ROW_TILES, BATCH, TASKS_PER_TILE]),
        )
        nc.vector.memset(select[B2_ROW : B2_ROW + 1, :, :], 1.0)

        G_ROW = EXPERTS * H_TILES
        B_ROW = G_ROW + EXPERTS * D_CHUNKS
        vec_rows = const.tile([P, P], BF16)
        nc.scalar.dma_start(out=vec_rows[0:G_ROW, :], in_=b1.rearrange("n (m q) -> (n m) q", q=P))
        nc.scalar.dma_start(out=vec_rows[G_ROW:B_ROW, :], in_=ln_g.rearrange("n (m q) -> (n m) q", q=P))
        nc.scalar.dma_start(out=vec_rows[B_ROW:P, :], in_=ln_b.rearrange("n (m q) -> (n m) q", q=P))
        b1_cols = const.tile([P, G_ROW], F32)
        gb_cols = const.tile([P, P - G_ROW], BF16)

        def transpose_vectors():
            vec_t = banks.tile([P, P], BF16, tag="bank")
            nc.tensor.transpose(vec_t[:], vec_rows[:], ident[:])
            nc.vector.tensor_copy(out=b1_cols[:], in_=vec_t[:, 0:G_ROW])
            nc.vector.tensor_copy(out=gb_cols[:], in_=vec_t[:, G_ROW:P])

        def spread_gain_beta(n):
            if n == EXPERTS - 1:
                gb = banks.tile([P, 2, D], BF16, tag="bank")
            else:
                gb = psum_gb.tile([P, 2, D], BF16)
            for which in range(2):
                for m in range(D_CHUNKS):
                    col = which * EXPERTS * D_CHUNKS + n * D_CHUNKS + m
                    nc.tensor.transpose(
                        gb[:, which, m * P : (m + 1) * P],
                        gb_cols[:, col : col + 1].to_broadcast([P, P]),
                        ident[:],
                    )
            tiles["gb", n] = gb

        def add_task_embedding(n):
            xs_bf = double.tile([P, ROW_TILES, D], BF16)
            nc.vector.tensor_tensor(out=xs_bf[:], in0=tiles["xm", n][:], in1=te_rep[:], op=ALU.add)
            x_words = double.tile([P, ROWS, 2], F32, align_bytes=64)
            tiles["xs_bf", n] = xs_bf
            tiles["x_words", n] = x_words

        def transpose_x(n, half):
            xt = banks.tile([P, TILES_PER_HALF, 2, P], F32, tag="bank")
            words = tiles["xs_bf", n][:].bitcast(F32)
            for i in range(TILES_PER_HALF):
                for u in range(2):
                    nc.tensor.transpose(
                        xt[:, i, u, :], words[:, half * TILES_PER_HALF + i, u * P : (u + 1) * P], ident_f32[:]
                    )
            tiles["xt", n, half] = xt

        def copy_x(n, half):
            rows = slice(half * TILES_PER_HALF * P, (half + 1) * TILES_PER_HALF * P)
            nc.scalar.copy(
                out=tiles["x_words", n][:, rows, :].rearrange("p (i r) u -> p i r u", i=TILES_PER_HALF),
                in_=tiles["xt", n, half][:].rearrange("p i u r -> p i r u"),
            )

        def quantise_x(n):
            x_codes = double.tile([P, ROWS], U32, align_bytes=64)
            x_scales = double.tile([P, ROWS], U8, align_bytes=64)
            nc.vector.quantize_mx(
                out=x_codes[:].bitcast(FP8X4),
                scales=x_scales[:],
                in_=tiles["x_words", n][:].rearrange("p r u -> p (r u)").bitcast(BF16),
            )
            tiles["x_codes", n] = x_codes
            tiles["x_scales", n] = x_scales

        def gpsimd_regroup(grouped, planes):
            nc.gpsimd.tensor_scalar(
                out=grouped.rearrange("p (c i) t -> p c t i", i=4),
                in0=planes.rearrange("p t (c i) -> p c t i", i=4),
                scalar1=1.0,
                scalar2=0.0,
                op0=ALU.mult,
                op1=ALU.add,
            )

        def new_grouped_weights(n):
            w1_grouped = single.tile([P, H, PACK], BF16, align_bytes=64)
            w2_grouped = single.tile([P, H_PASSES, D, PACK], BF16, align_bytes=64)
            tiles["w1_grouped", n] = w1_grouped
            tiles["w2_grouped", n] = w2_grouped

        def regroup_w1(n, engine, first, count):
            cols = slice(first, first + count)
            grouped = tiles["w1_grouped", n][:, cols, :]
            planes = tiles["w1_raw", n][:, :, cols]
            if engine == "gpsimd":
                gpsimd_regroup(grouped, planes)
            elif engine == "vector":
                regroup(nc.vector.tensor_copy, grouped, planes)
            else:
                regroup(nc.scalar.copy, grouped, planes)

        def regroup_w2(n, engine, c, first=0, count=D):
            cols = slice(first, first + count)
            grouped = tiles["w2_grouped", n][:, c, cols, :]
            planes = tiles["w2_raw", n][:, c, :, cols]
            if engine == "gpsimd":
                gpsimd_regroup(grouped, planes)
            elif engine == "vector":
                regroup(nc.vector.tensor_copy, grouped, planes)
            else:
                regroup(nc.scalar.copy, grouped, planes)

        def quantise_w1(n):
            w1_codes = double.tile([P, H], U32, align_bytes=64)
            w1_scales = double.tile([P, H], U8, align_bytes=64)
            nc.vector.quantize_mx(
                out=w1_codes[:].bitcast(FP8X4),
                scales=w1_scales[:],
                in_=tiles["w1_grouped", n][:].rearrange("p w t -> p (w t)"),
            )
            tiles["w1_codes", n] = w1_codes
            tiles["w1_scales", n] = w1_scales

        def quantise_w2(n):
            w2_codes = double.tile([P, H_PASSES, D], U32, align_bytes=64)
            w2_scales = double.tile([P, H_PASSES, D], U8, align_bytes=64)
            nc.vector.quantize_mx(
                out=w2_codes[:].rearrange("p c w -> p (c w)").bitcast(FP8X4),
                scales=w2_scales[:].rearrange("p c w -> p (c w)"),
                in_=tiles["w2_grouped", n][:].rearrange("p c w t -> p (c w t)"),
            )
            tiles["w2_codes", n] = w2_codes
            tiles["w2_scales", n] = w2_scales

        def shift_rows(n, i):
            shift = banks.tile([P, D], F32, tag="bank")
            nc.tensor.matmul(out=shift[:], lhsT=select[:, i, :], rhs=addends[:, n, :], start=True, stop=True)
            tiles["shift", n, i] = shift

        def new_residual_addend(n):
            resid = triple.tile([P, ROW_TILES, D], F32)
            tiles["resid", n] = resid

        def residual_addend(n, i):
            nc.vector.tensor_tensor(
                out=tiles["resid", n][:, i, :], in0=tiles["shift", n, i][:], in1=tiles["xm", n][:, i, :], op=ALU.add
            )

        def hidden_units(n, first, count):
            if first == 0:
                h_t = single.tile([P, H_TILES, ROWS], BF16)
                tiles["h_t", n] = h_t
            for m in range(first, first + count):
                units = slice(m * P, (m + 1) * P)
                pre = banks.tile([P, ROWS], F32, tag="bank")
                nc.tensor.matmul_mx(
                    out=pre[:],
                    lhsT=tiles["w1_codes", n][:, units].bitcast(FP8X4),
                    lhsT_scale=tiles["w1_scales", n][:, units],
                    rhs=tiles["x_codes", n][:].bitcast(FP8X4),
                    rhs_scale=tiles["x_scales", n][:],
                    start=True,
                    stop=True,
                )
                tiles["pre", n, m] = pre

        def silu(n, first, count):
            for m in range(first, first + count):
                col = n * H_TILES + m
                nc.scalar.activation(
                    out=tiles["h_t", n][:, m, :],
                    in_=tiles["pre", n, m][:],
                    func=ACT.Silu,
                    bias=b1_cols[:, col : col + 1],
                    scale=1.0,
                )

        def regroup_h(n, engine, c):
            h_grouped = double.tile([P, ROWS, PACK], BF16, align_bytes=64)
            planes = tiles["h_t", n][:, c * PACK : (c + 1) * PACK, :]
            if engine == "gpsimd":
                gpsimd_regroup(h_grouped[:], planes)
            else:
                regroup(nc.scalar.copy, h_grouped[:], planes)
            tiles["h_grouped", n, c] = h_grouped

        def quantise_h(n, c):
            if c == 0:
                h_codes = double.tile([P, H_PASSES, ROWS], U32, align_bytes=64)
                h_scales = double.tile([P, H_PASSES, ROWS], U8, align_bytes=64)
                tiles["h_codes", n] = h_codes
                tiles["h_scales", n] = h_scales
            nc.vector.quantize_mx(
                out=tiles["h_codes", n][:, c, :].bitcast(FP8X4),
                scales=tiles["h_scales", n][:, c, :],
                in_=tiles["h_grouped", n, c][:].rearrange("p r t -> p (r t)"),
            )

        def second_product(n, i):
            rows = slice(i * P, (i + 1) * P)
            mlp = banks.tile([P, D], F32, tag="bank")
            for c in range(H_PASSES):
                nc.tensor.matmul_mx(
                    out=mlp[:],
                    lhsT=tiles["h_codes", n][:, c, rows].bitcast(FP8X4),
                    lhsT_scale=tiles["h_scales", n][:, c, rows],
                    rhs=tiles["w2_codes", n][:, c, :].bitcast(FP8X4),
                    rhs_scale=tiles["w2_scales", n][:, c, :],
                    start=(c == 0),
                    stop=(c == H_PASSES - 1),
                )
            tiles["mlp", n, i] = mlp

        def residual_sum(n, i):
            if i == 0:
                r_sum = triple.tile([P, ROW_TILES], F32)
                neg_mean = triple.tile([P, ROW_TILES], F32)
                sq_sum = triple.tile([P, ROW_TILES], F32)
                tiles["r_sum", n] = r_sum
                tiles["neg_mean", n] = neg_mean
                tiles["sq_sum", n] = sq_sum
            r = rows_pool.tile([P, D], F32)
            nc.vector.scalar_tensor_tensor(
                out=r[:],
                in0=tiles["mlp", n, i][:],
                scalar=1.0,
                in1=tiles["resid", n][:, i, :],
                op0=ALU.mult,
                op1=ALU.add,
                accum_out=tiles["r_sum", n][:, i : i + 1],
            )
            tiles["r", n, i] = r

        def squared_deviations(n, half):
            cols = slice(half * TILES_PER_HALF, (half + 1) * TILES_PER_HALF)
            nc.scalar.activation(
                out=tiles["neg_mean", n][:, cols], in_=tiles["r_sum", n][:, cols], func=ACT.Copy, scale=-1.0 / D
            )
            for i in range(cols.start, cols.stop):
                squares = double.tile([P, D], BF16)
                nc.scalar.activation(
                    out=squares[:],
                    in_=tiles["r", n, i][:],
                    func=ACT.Square,
                    bias=tiles["neg_mean", n][:, i : i + 1],
                    scale=1.0,
                    accum_out=tiles["sq_sum", n][:, i : i + 1],
                )

        def inverse_deviation(n):
            var_eps = triple.tile([P, ROW_TILES], F32)
            nc.gpsimd.tensor_scalar(
                out=var_eps[:], in0=tiles["sq_sum", n][:], scalar1=1.0 / D, scalar2=LN_EPS, op0=ALU.mult, op1=ALU.add
            )
            rstd = triple.tile([P, ROW_TILES], F32)
            nc.gpsimd.tensor_tensor(out=rstd[:], in0=var_eps[:], in1=neg_half[:], op=ALU.pow)
            tiles["rstd", n] = rstd

        def centre_and_gain(n, i):
            centred_gain = norm.tile([P, D], F32)
            nc.vector.scalar_tensor_tensor(
                out=centred_gain[:],
                in0=tiles["r", n, i][:],
                scalar=tiles["neg_mean", n][:, i : i + 1],
                in1=tiles["gb", n][:, 0, :],
                op0=ALU.add,
                op1=ALU.mult,
            )
            tiles["centred_gain", n, i] = centred_gain

        def store_rows(n, first, count, y):
            for j in range(TASKS_PER_TILE):
                nc.sync.dma_start(
                    out=task_rows(out[:, n], j)[:, first : first + count, :],
                    in_=y[j:P:TASKS_PER_TILE, :, :],
                )

        def finish(n, first, count):
            y = norm.tile([P, TILES_PER_HALF, D], F32)
            for k in range(count):
                nc.vector.scalar_tensor_tensor(
                    out=y[:, k, :],
                    in0=tiles["centred_gain", n, first + k][:],
                    scalar=tiles["rstd", n][:, first + k : first + k + 1],
                    in1=tiles["gb", n][:, 1, :],
                    op0=ALU.mult,
                    op1=ALU.add,
                )
            store_rows(n, first, count, y[:, 0:count, :])

        def load_gain_beta(n):
            gain_sb = triple.tile([P, D], BF16)
            nc.sync.dma_start(out=gain_sb[:], in_=ln_g[n].partition_broadcast(P))
            beta_sb = triple.tile([P, D], BF16)
            nc.sync.dma_start(out=beta_sb[:], in_=ln_b[n].partition_broadcast(P))
            tiles["gain_sb", n] = gain_sb
            tiles["beta_sb", n] = beta_sb

        def gpsimd_finish(n, i):
            scratch = single.tile([P, 2, D], F32, tag="w2_grouped", align_bytes=64)
            z = scratch[:, 0, :]
            z_gain = scratch[:, 1, :]
            nc.gpsimd.tensor_scalar(
                out=z,
                in0=tiles["r", n, i][:],
                scalar1=tiles["neg_mean", n][:, i : i + 1],
                scalar2=tiles["rstd", n][:, i : i + 1],
                op0=ALU.add,
                op1=ALU.mult,
            )
            nc.gpsimd.tensor_tensor(out=z_gain, in0=z, in1=tiles["gain_sb", n][:], op=ALU.mult)
            y_one = double.tile([P, 1, D], F32)
            nc.gpsimd.tensor_tensor(out=y_one[:, 0, :], in0=z_gain, in1=tiles["beta_sb", n][:], op=ALU.add)
            store_rows(n, i, 1, y_one[:])

        def is_expert(n):
            return 0 <= n < EXPERTS

        def gpsimd_finishes(n):
            return is_expert(n) and not is_expert(n + 3) and is_expert(n + 1)

        add_task_embedding(0)
        transpose_x(0, 0)
        transpose_x(0, 1)
        new_grouped_weights(0)
        regroup_w1(0, "vector", 0, H // 2)
        copy_x(0, 0)
        copy_x(0, 1)
        regroup_w1(0, "vector", H // 2, H // 2)
        transpose_vectors()

        for r in range(EXPERTS + 2):
            following, this, before, last = r + 1, r, r - 1, r - 2
            vector_halves = max(0, 2 - r)
            gpsimd_tiles = 1 if gpsimd_finishes(last) else 0
            vector_tiles = ROW_TILES - gpsimd_tiles
            if is_expert(r + 2):
                load(r + 2)
            if gpsimd_finishes(this):
                load_gain_beta(this)
            if is_expert(this):
                quantise_x(this)
                quantise_w1(this)
                hidden_units(this, 0, 4)
            if is_expert(before):
                quantise_h(before, 0)
                quantise_h(before, 1)
            if before >= 1 and is_expert(before):
                second_product(before, 0)
                second_product(before, 1)
            if following >= 3 and is_expert(following):
                shift_rows(following, 0)
                shift_rows(following, 1)
            if is_expert(this):
                hidden_units(this, 4, 4)
                silu(this, 0, H_TILES)
            if is_expert(following):
                add_task_embedding(following)
            if this == 0:
                regroup_w2(this, "vector", 0)
                regroup_w2(this, "vector", 1)
            if is_expert(this):
                quantise_w2(this)
            if is_expert(following):
                new_grouped_weights(following)
                regroup_w2(following, "gpsimd", 0)
                for s in range(2 - vector_halves):
                    regroup_w1(following, "gpsimd", s * (H // 2), H // 2)
                regroup_w2(following, "gpsimd", 1, 0, W2_COLS_GPSIMD)
            if gpsimd_tiles >= 1:
                gpsimd_finish(last, ROW_TILES - 1)
            if this == 0:
                new_residual_addend(this)
                shift_rows(following, 0)
                shift_rows(following, 1)

            if before == 0:
                for i in range(ROW_TILES):
                    shift_rows(before, i)
                    residual_addend(before, i)
                second_product(before, 0)
                second_product(before, 1)
                shift_rows(following, 0)
                shift_rows(following, 1)
            if is_expert(last) and not is_expert(this):
                for i in range(vector_tiles):
                    centre_and_gain(last, i)
            if is_expert(before):
                residual_sum(before, 0)
                residual_sum(before, 1)
                second_product(before, 2)
                second_product(before, 3)
            if is_expert(following):
                new_residual_addend(following)
                residual_addend(following, 0)
                residual_addend(following, 1)
                shift_rows(following, 2)
                shift_rows(following, 3)
                transpose_x(following, 0)
                transpose_x(following, 1)
            if is_expert(this):
                regroup_h(this, "scalar", 0)
                if not is_expert(following):
                    regroup_h(this, "gpsimd", 1)
            if is_expert(before):
                residual_sum(before, 2)
                residual_sum(before, 3)
            if before == EXPERTS - 1:
                spread_gain_beta(before)
            if is_expert(following):
                residual_addend(following, 2)
                residual_addend(following, 3)
                for s in range(2 - vector_halves, 2):
                    regroup_w1(following, "vector", s * (H // 2), H // 2)
            if is_expert(before):
                squared_deviations(before, 0)
                squared_deviations(before, 1)
                inverse_deviation(before)
            if is_expert(following):
                copy_x(following, 0)
                copy_x(following, 1)
                regroup_h(this, "scalar", 1)
                regroup_w2(following, "scalar", 1, W2_COLS_GPSIMD, D - W2_COLS_GPSIMD)
            if is_expert(last):
                if is_expert(this):
                    for i in range(vector_tiles):
                        centre_and_gain(last, i)
                finish(last, 0, TILES_PER_HALF)
                finish(last, TILES_PER_HALF, vector_tiles - TILES_PER_HALF)
            if is_expert(before) and before < EXPERTS - 1:
                spread_gain_beta(before)
